import numpy as np
import ml_dtypes

BF16 = ml_dtypes.bfloat16


def bf(x):
    return np.asarray(x, np.float32).astype(BF16)


def f32(x):
    return np.asarray(x, np.float32)


def f64(x):
    return np.asarray(x).astype(np.float64)


def striped(idx):
    return np.tile(idx.reshape(-1, 16).T, (8, 1))


C, S, N, K, H, F = 384, 1024, 1536, 3, 512, 1536
EPS_R, EPS_L = 1e-8, 1e-6


def gelu_tanh(v):
    return 0.5 * v * (1.0 + np.tanh(np.sqrt(2.0 / np.pi) * (v + 0.044715 * v**3)))


def rmsnorm(x):
    return x / (np.sqrt((x**2).mean(0, keepdims=True)) + EPS_R)


def layernorm(x, a, b):
    mu = x.mean(0, keepdims=True)
    sd = np.sqrt(((x - mu) ** 2).mean(0, keepdims=True))
    return a * (x - mu) / (sd + EPS_L) + b


def setup_inputs():
    r = np.random.standard_normal
    return {
        "emb": f32(r((C, S))),
        "hidden": f32(r((C, N))),
        "w_fut": bf(r((C, C)) / np.sqrt(2.0 * C)),
        "w_hid": bf(r((C, C)) / np.sqrt(2.0 * C)),
        "proj_b": f32(0.1 * r((C, 1))),
        "ln1_a": f32(1.0 + 0.1 * r((C, 1))),
        "ln1_b": f32(0.1 * r((C, 1))),
        "w_v": bf(r((C, C)) / np.sqrt(C)),
        "b_v": f32(0.1 * r((C, 1))),
        "w_o": bf(r((C, C)) / np.sqrt(C)),
        "b_o": f32(0.1 * r((C, 1))),
        "ln2_a": f32(1.0 + 0.1 * r((C, 1))),
        "ln2_b": f32(0.1 * r((C, 1))),
        "fc_w": bf(r((C, F)) / np.sqrt(C)),
        "fc_b": f32(0.1 * r((F, 1))),
        "fcp_w": bf(r((F, C)) / np.sqrt(F)),
        "fcp_b": f32(0.1 * r((C, 1))),
        "unembd_w": bf(r((C, S)) / np.sqrt(C)),
        "unembd_b": f32(0.1 * r((S, 1))),
        "offs": striped(np.concatenate([np.random.permutation(S)[:H] for _ in range(K)])),
    }


def reference(emb, hidden, w_fut, w_hid, proj_b, ln1_a, ln1_b, w_v, b_v, w_o, b_o, ln2_a, ln2_b, fc_w, fc_b, fcp_w, fcp_b, unembd_w, unembd_b, offs):
    idx = offs[:16].T.reshape(-1)
    p = f64(w_fut).T @ rmsnorm(f64(emb))
    q = f64(w_hid).T @ rmsnorm(f64(hidden)) + f64(proj_b)
    curr = p[:, idx] + q
    xn = layernorm(curr, f64(ln1_a), f64(ln1_b))
    v = f64(w_v).T @ xn + f64(b_v)
    x1 = curr + f64(w_o).T @ v + f64(b_o)
    xn2 = layernorm(x1, f64(ln2_a), f64(ln2_b))
    h = gelu_tanh(f64(fc_w).T @ xn2 + f64(fc_b))
    x2 = x1 + f64(fcp_w).T @ h + f64(fcp_b)
    return f64(unembd_w).T @ x2 + f64(unembd_b)

@@ -1,0 +1,201 @@
+import concourse.masks as masks
+import concourse.mybir as mybir
+
+F32, BF16, U16 = mybir.dt.float32, mybir.dt.bfloat16, mybir.dt.uint16
+ALU = mybir.AluOpType
+ACT = mybir.ActivationFunctionType
+
+P = 128
+C, S, N, F = 384, 1024, 1536, 1536
+CB, SB, FB = C // P, S // P, F // P
+BANK = 512
+CHUNK = 512
+EPS_RMS, EPS_LN = 1e-8, 1e-6
+
+FLOPS = 2 * (C * C * S + 3 * C * C * N + 2 * C * F * N + C * S * N)
+
+
+def tile_mtp_b_kernel(
+    tc, emb, hidden, w_fut, w_hid, proj_b, ln1_a, ln1_b, w_v, b_v, w_o, b_o,
+    ln2_a, ln2_b, fc_w, fc_b, fcp_w, fcp_b, unembd_w, unembd_b, offs, out,
+):
+    nc = tc.nc
+    with (
+        tc.tile_pool(name="held", bufs=1) as held,
+        tc.tile_pool(name="work", bufs=2) as work,
+        tc.tile_pool(name="kept", bufs=3) as kept,
+        tc.tile_pool(name="turned", bufs=2 * CHUNK // P) as turned,
+        tc.tile_pool(name="small", bufs=8) as small,
+        tc.tile_pool(name="logits", bufs=4) as logits,
+        tc.psum_pool(name="to_tokens", bufs=2) as to_tokens,
+        tc.psum_pool(name="to_channels", bufs=2) as to_channels,
+        tc.psum_pool(name="products", bufs=4) as products,
+    ):
+        offsets = held.tile([P, N // 16], U16, name="offsets")
+        nc.sync.dma_start(offsets[:], offs)
+
+        def load_weights(w, name):
+            tile = held.tile([P, w.shape[0] // P, w.shape[1]], BF16, name=name)
+            nc.sync.dma_start(tile[:], w.rearrange("(kb p) m -> p kb m", p=P))
+            return tile
+
+        emb_sb = held.tile([P, CB, S], F32, name="emb_sb")
+        for s0 in range(0, S, BANK):
+            for b in range(CB):
+                nc.sync.dma_start(emb_sb[:, b, s0 : s0 + BANK], emb[b * P : (b + 1) * P, s0 : s0 + BANK])
+        w_fut_sb = load_weights(w_fut, "w_fut_sb")
+        hidden_sb = held.tile([P, CB, N], F32, name="hidden_sb")
+
+        def load_hidden(t0):
+            for b in range(CB):
+                nc.sync.dma_start(hidden_sb[:, b, t0 : t0 + CHUNK], hidden[b * P : (b + 1) * P, t0 : t0 + CHUNK])
+
+        load_hidden(0)
+        w_hid_sb = load_weights(w_hid, "w_hid_sb")
+        w_v_sb = load_weights(w_v, "w_v_sb")
+        w_o_sb = load_weights(w_o, "w_o_sb")
+        for t0 in range(CHUNK, N, CHUNK):
+            load_hidden(t0)
+        fc_w_sb = load_weights(fc_w, "fc_w_sb")
+        fcp_w_sb = load_weights(fcp_w, "fcp_w_sb")
+        unembd_w_sb = load_weights(unembd_w, "unembd_w_sb")
+
+        ident_f32 = held.tile([P, P], F32, name="ident_f32")
+        masks.make_identity(nc, ident_f32[:])
+        ident_bf16 = held.tile([P, P], BF16, name="ident_bf16")
+        masks.make_identity(nc, ident_bf16[:])
+        half = held.tile([P, 1], F32, name="half")
+        nc.gpsimd.memset(half[:], 0.5)
+
+        vectors = {
+            "proj_b": proj_b, "ln1_a": ln1_a, "ln1_b": ln1_b, "b_v": b_v, "b_o": b_o, "ln2_a": ln2_a,
+            "ln2_b": ln2_b, "fcp_b": fcp_b, "fc_b": fc_b, "unembd_b": unembd_b,
+        }
+        first_row = {}
+        n_rows = 0
+        for name, vec in vectors.items():
+            first_row[name] = n_rows
+            n_rows += vec.shape[0] // P
+        rows = held.tile([n_rows, P], F32, name="rows")
+        for name, vec in vectors.items():
+            r0 = first_row[name]
+            nc.scalar.dma_start(rows[r0 : r0 + vec.shape[0] // P, :], vec.rearrange("(b p) o -> b (p o)", p=P))
+        columns_ps = to_tokens.tile([P, n_rows], F32, tag="tokens_ps")
+        nc.tensor.transpose(columns_ps[:], rows[:], ident_f32[0:n_rows, 0:n_rows])
+        columns = held.tile([P, n_rows], F32, name="columns")
+        nc.vector.tensor_copy(columns[:], columns_ps[:])
+
+        def column(name, block):
+            c = first_row[name] + block
+            return columns[:, c : c + 1]
+
+        def normalise(x, y, eps, gain=None, shift=None):
+            layer_norm = gain is not None
+            width = x[0].shape[1]
+            turned_dt = F32 if layer_norm else BF16
+            ident = ident_f32 if layer_norm else ident_bf16
+            scaled = []
+            for g in range(width // P):
+                tokens_ps = to_tokens.tile([P, C], F32, name="tokens_ps")
+                for b in range(CB):
+                    nc.tensor.transpose(tokens_ps[:, b * P : (b + 1) * P], x[b][:, g * P : (g + 1) * P], ident_f32[:])
+                stats = small.tile([P, 6], F32, name="stats")
+                nc.vector.bn_stats(stats[:], tokens_ps[:])
+                mean_var = small.tile([P, 2], F32, name="mean_var")
+                nc.vector.bn_aggr(mean_var[:], stats[:])
+                mean, var = mean_var[:, 0:1], mean_var[:, 1:2]
+                if layer_norm:
+                    spread2 = var
+                else:
+                    mean_sq = small.tile([P, 1], F32, name="mean_sq")
+                    nc.vector.scalar_tensor_tensor(mean_sq[:], mean, mean, var, ALU.mult, ALU.add)
+                    spread2 = mean_sq[:]
+                spread = small.tile([P, 1], F32, name="spread")
+                nc.gpsimd.tensor_tensor(spread[:], spread2, half[:], ALU.pow)
+                inverse = small.tile([P, 1], F32, name="inverse")
+                nc.vector.tensor_scalar_add(inverse[:], spread[:], eps)
+                nc.vector.reciprocal(inverse[:], inverse[:])
+                tokens = turned.tile([P, C], turned_dt, name="tokens_f32" if layer_norm else "tokens_bf16")
+                if layer_norm:
+                    nc.vector.tensor_scalar(tokens[:], tokens_ps[:], mean, inverse[:], ALU.subtract, ALU.mult)
+                else:
+                    nc.scalar.activation(tokens[:], tokens_ps[:], ACT.Identity, scale=inverse[:])
+                scaled.append(tokens)
+            for b in range(CB):
+                channels_ps = to_channels.tile([P, width], turned_dt, name="channels_ps")
+                for g in range(width // P):
+                    nc.tensor.transpose(channels_ps[:, g * P : (g + 1) * P], scaled[g][:, b * P : (b + 1) * P], ident[:])
+                if layer_norm:
+                    nc.scalar.activation(
+                        y[b], channels_ps[:], ACT.Identity, bias=column(shift, b), scale=column(gain, b)
+                    )
+                else:
+                    nc.scalar.copy(y[b], channels_ps[:])
+
+        def project(w_sb, m, x):
+            product = products.tile([P, x[0].shape[1]], F32, name="product")
+            for kb in range(len(x)):
+                nc.tensor.matmul(
+                    product[:], w_sb[:, kb, m * P : (m + 1) * P], x[kb], start=(kb == 0), stop=(kb == len(x) - 1)
+                )
+            return product
+
+        def blocks(tile):
+            return [tile[:, b, :] for b in range(tile.shape[1])]
+
+        e = held.tile([P, CB, S], BF16, name="e")
+        table = [held.tile([P, S], F32, name=f"table{m}") for m in range(CB)]
+        for s0 in range(0, S, BANK):
+            e_piece = [e[:, b, s0 : s0 + BANK] for b in range(CB)]
+            normalise([emb_sb[:, b, s0 : s0 + BANK] for b in range(CB)], e_piece, EPS_RMS)
+            for m in range(CB):
+                nc.scalar.copy(table[m][:, s0 : s0 + BANK], project(w_fut_sb, m, e_piece)[:])
+
+        def attention_block(t0):
+            u = work.tile([P, CB, CHUNK], BF16, name="u")
+            normalise([hidden_sb[:, b, t0 : t0 + CHUNK] for b in range(CB)], blocks(u), EPS_RMS)
+            q = work.tile([P, CB, CHUNK], F32, name="q")
+            curr = work.tile([P, CB, CHUNK], F32, name="curr")
+            piece = offsets[:, t0 // 16 : (t0 + CHUNK) // 16]
+            for m in range(CB):
+                nc.scalar.activation(q[:, m, :], project(w_hid_sb, m, blocks(u))[:], ACT.Identity, bias=column("proj_b", m))
+                nc.vector.tensor_tensor(curr[:, m, :], table[m][:].indirect(piece), q[:, m, :], ALU.add)
+            xn = work.tile([P, CB, CHUNK], BF16, name="xn")
+            normalise(blocks(curr), blocks(xn), EPS_LN, "ln1_a", "ln1_b")
+            v = work.tile([P, CB, CHUNK], BF16, name="v")
+            for m in range(CB):
+                nc.scalar.activation(v[:, m, :], project(w_v_sb, m, blocks(xn))[:], ACT.Identity, bias=column("b_v", m))
+            x1 = kept.tile([P, CB, CHUNK], F32, name="x1")
+            for m in range(CB):
+                nc.vector.scalar_tensor_tensor(
+                    x1[:, m, :], project(w_o_sb, m, blocks(v))[:], column("b_o", m), curr[:, m, :], ALU.add, ALU.add
+                )
+            xn2 = kept.tile([P, CB, CHUNK], BF16, name="xn2")
+            normalise(blocks(x1), blocks(xn2), EPS_LN, "ln2_a", "ln2_b")
+            return x1, xn2
+
+        def mlp_and_logits(t0, x1, xn2):
+            h = work.tile([P, FB, CHUNK], BF16, name="h")
+            for f in range(FB):
+                nc.scalar.activation(
+                    h[:, f, :], project(fc_w_sb, f, blocks(xn2))[:], ACT.Gelu_apprx_tanh, bias=column("fc_b", f)
+                )
+            x2 = work.tile([P, CB, CHUNK], BF16, name="x2")
+            for m in range(CB):
+                nc.vector.scalar_tensor_tensor(
+                    x2[:, m, :], project(fcp_w_sb, m, blocks(h))[:], column("fcp_b", m), x1[:, m, :], ALU.add, ALU.add
+                )
+            for t in range(SB):
+                logit = logits.tile([P, CHUNK], F32, name="logit")
+                nc.scalar.activation(
+                    logit[:], project(unembd_w_sb, t, blocks(x2))[:], ACT.Identity, bias=column("unembd_b", t)
+                )
+                nc.sync.dma_start(out[t * P : (t + 1) * P, t0 : t0 + CHUNK], logit[:])
+
+        starts = list(range(0, N, CHUNK))
+        ready = {starts[0]: attention_block(starts[0])}
+        for t0 in starts:
+            if t0 + CHUNK < N:
+                ready[t0 + CHUNK] = attention_block(t0 + CHUNK)
+            x1, xn2 = ready[t0]
+            mlp_and_logits(t0, x1, xn2)

@@ -8,7 +8,6 @@ ACT = mybir.ActivationFunctionType
 P = 128
 C, S, N, F = 384, 1024, 1536, 1536
 CB, SB, FB = C // P, S // P, F // P
-BANK = 512
 CHUNK = 512
 EPS_RMS, EPS_LN = 1e-8, 1e-6
 
@@ -20,19 +19,23 @@ def tile_mtp_b_kernel(
     ln2_a, ln2_b, fc_w, fc_b, fcp_w, fcp_b, unembd_w, unembd_b, offs, out,
 ):
     nc = tc.nc
+    chunks = list(range(0, N, CHUNK))
     with (
         tc.tile_pool(name="held", bufs=1) as held,
-        tc.tile_pool(name="work", bufs=2) as work,
-        tc.tile_pool(name="kept", bufs=3) as kept,
-        tc.tile_pool(name="turned", bufs=2 * CHUNK // P) as turned,
-        tc.tile_pool(name="small", bufs=8) as small,
+        tc.tile_pool(name="stream", bufs=len(chunks)) as stream,
+        tc.tile_pool(name="operands", bufs=len(chunks) + 1) as operands,
+        tc.tile_pool(name="scratch", bufs=3) as scratch,
+        tc.tile_pool(name="wide", bufs=2) as wide,
         tc.tile_pool(name="logits", bufs=4) as logits,
-        tc.psum_pool(name="to_tokens", bufs=2) as to_tokens,
-        tc.psum_pool(name="to_channels", bufs=2) as to_channels,
-        tc.psum_pool(name="products", bufs=4) as products,
+        tc.psum_pool(name="means", bufs=2) as means,
+        tc.psum_pool(name="products", bufs=6) as products,
     ):
         offsets = held.tile([P, N // 16], U16, name="offsets")
         nc.sync.dma_start(offsets[:], offs)
+
+        def load_columns(tile, source, c0):
+            for b in range(CB):
+                nc.sync.dma_start(tile[:, b, c0 : c0 + CHUNK], source[b * P : (b + 1) * P, c0 : c0 + CHUNK])
 
         def load_weights(w, name):
             tile = held.tile([P, w.shape[0] // P, w.shape[1]], BF16, name=name)
@@ -40,32 +43,29 @@ def tile_mtp_b_kernel(
             return tile
 
         emb_sb = held.tile([P, CB, S], F32, name="emb_sb")
-        for s0 in range(0, S, BANK):
-            for b in range(CB):
-                nc.sync.dma_start(emb_sb[:, b, s0 : s0 + BANK], emb[b * P : (b + 1) * P, s0 : s0 + BANK])
-        w_fut_sb = load_weights(w_fut, "w_fut_sb")
         hidden_sb = held.tile([P, CB, N], F32, name="hidden_sb")
-
-        def load_hidden(t0):
-            for b in range(CB):
-                nc.sync.dma_start(hidden_sb[:, b, t0 : t0 + CHUNK], hidden[b * P : (b + 1) * P, t0 : t0 + CHUNK])
-
-        load_hidden(0)
+        for s0 in range(0, S, CHUNK):
+            load_columns(emb_sb, emb, s0)
+        w_fut_sb = load_weights(w_fut, "w_fut_sb")
+        for t0 in chunks:
+            load_columns(hidden_sb, hidden, t0)
         w_hid_sb = load_weights(w_hid, "w_hid_sb")
         w_v_sb = load_weights(w_v, "w_v_sb")
         w_o_sb = load_weights(w_o, "w_o_sb")
-        for t0 in range(CHUNK, N, CHUNK):
-            load_hidden(t0)
         fc_w_sb = load_weights(fc_w, "fc_w_sb")
         fcp_w_sb = load_weights(fcp_w, "fcp_w_sb")
         unembd_w_sb = load_weights(unembd_w, "unembd_w_sb")
 
-        ident_f32 = held.tile([P, P], F32, name="ident_f32")
-        masks.make_identity(nc, ident_f32[:])
-        ident_bf16 = held.tile([P, P], BF16, name="ident_bf16")
-        masks.make_identity(nc, ident_bf16[:])
-        half = held.tile([P, 1], F32, name="half")
-        nc.gpsimd.memset(half[:], 0.5)
+        mean_w = held.tile([P, P], F32, name="mean_w")
+        nc.vector.memset(mean_w[:], 1.0 / C)
+        minus_mean_w = held.tile([P, P], F32, name="minus_mean_w")
+        nc.vector.memset(minus_mean_w[:], -1.0 / C)
+        eps_rms = held.tile([P, 1], F32, name="eps_rms")
+        nc.vector.memset(eps_rms[:], EPS_RMS)
+        eps_ln = held.tile([P, 1], F32, name="eps_ln")
+        nc.vector.memset(eps_ln[:], EPS_LN)
+        ident = held.tile([P, P], F32, name="ident")
+        masks.make_identity(nc, ident[:])
 
         vectors = {
             "proj_b": proj_b, "ln1_a": ln1_a, "ln1_b": ln1_b, "b_v": b_v, "b_o": b_o, "ln2_a": ln2_a,
@@ -80,8 +80,8 @@ def tile_mtp_b_kernel(
         for name, vec in vectors.items():
             r0 = first_row[name]
             nc.scalar.dma_start(rows[r0 : r0 + vec.shape[0] // P, :], vec.rearrange("(b p) o -> b (p o)", p=P))
-        columns_ps = to_tokens.tile([P, n_rows], F32, tag="tokens_ps")
-        nc.tensor.transpose(columns_ps[:], rows[:], ident_f32[0:n_rows, 0:n_rows])
+        columns_ps = means.tile([P, n_rows], F32, tag="mean_ps")
+        nc.tensor.transpose(columns_ps[:], rows[:], ident[0:n_rows, 0:n_rows])
         columns = held.tile([P, n_rows], F32, name="columns")
         nc.vector.tensor_copy(columns[:], columns_ps[:])
 
@@ -89,113 +89,113 @@ def tile_mtp_b_kernel(
             c = first_row[name] + block
             return columns[:, c : c + 1]
 
-        def normalise(x, y, eps, gain=None, shift=None):
-            layer_norm = gain is not None
-            width = x[0].shape[1]
-            turned_dt = F32 if layer_norm else BF16
-            ident = ident_f32 if layer_norm else ident_bf16
-            scaled = []
-            for g in range(width // P):
-                tokens_ps = to_tokens.tile([P, C], F32, name="tokens_ps")
-                for b in range(CB):
-                    nc.tensor.transpose(tokens_ps[:, b * P : (b + 1) * P], x[b][:, g * P : (g + 1) * P], ident_f32[:])
-                stats = small.tile([P, 6], F32, name="stats")
-                nc.vector.bn_stats(stats[:], tokens_ps[:])
-                mean_var = small.tile([P, 2], F32, name="mean_var")
-                nc.vector.bn_aggr(mean_var[:], stats[:])
-                mean, var = mean_var[:, 0:1], mean_var[:, 1:2]
-                if layer_norm:
-                    spread2 = var
-                else:
-                    mean_sq = small.tile([P, 1], F32, name="mean_sq")
-                    nc.vector.scalar_tensor_tensor(mean_sq[:], mean, mean, var, ALU.mult, ALU.add)
-                    spread2 = mean_sq[:]
-                spread = small.tile([P, 1], F32, name="spread")
-                nc.gpsimd.tensor_tensor(spread[:], spread2, half[:], ALU.pow)
-                inverse = small.tile([P, 1], F32, name="inverse")
-                nc.vector.tensor_scalar_add(inverse[:], spread[:], eps)
-                nc.vector.reciprocal(inverse[:], inverse[:])
-                tokens = turned.tile([P, C], turned_dt, name="tokens_f32" if layer_norm else "tokens_bf16")
-                if layer_norm:
-                    nc.vector.tensor_scalar(tokens[:], tokens_ps[:], mean, inverse[:], ALU.subtract, ALU.mult)
-                else:
-                    nc.scalar.activation(tokens[:], tokens_ps[:], ACT.Identity, scale=inverse[:])
-                scaled.append(tokens)
+        def channel_mean(x, weights):
+            pair = scratch.tile([P, CHUNK], F32, name="pair")
+            nc.gpsimd.tensor_tensor(pair[:], x[0], x[1], ALU.add)
+            total = scratch.tile([P, CHUNK], F32, name="total")
+            nc.gpsimd.tensor_tensor(total[:], pair[:], x[2], ALU.add)
+            mean_ps = means.tile([P, CHUNK], F32, name="mean_ps")
+            nc.tensor.matmul(mean_ps[:], weights[:], total[:], start=True, stop=True)
+            return mean_ps
+
+        def inverse_spread(x, eps):
+            squares = scratch.tile([P, CB, CHUNK], F32, name="squares")
             for b in range(CB):
-                channels_ps = to_channels.tile([P, width], turned_dt, name="channels_ps")
-                for g in range(width // P):
-                    nc.tensor.transpose(channels_ps[:, g * P : (g + 1) * P], scaled[g][:, b * P : (b + 1) * P], ident[:])
-                if layer_norm:
-                    nc.scalar.activation(
-                        y[b], channels_ps[:], ACT.Identity, bias=column(shift, b), scale=column(gain, b)
-                    )
-                else:
-                    nc.scalar.copy(y[b], channels_ps[:])
+                nc.scalar.activation(squares[:, b, :], x[b], ACT.Square)
+            mean_ps = channel_mean(blocks(squares), mean_w)
+            inverse = scratch.tile([P, CHUNK], F32, name="inverse")
+            nc.scalar.activation(inverse[:], mean_ps[:], ACT.Sqrt)
+            nc.scalar.activation(inverse[:], inverse[:], ACT.Square, bias=eps[:])
+            nc.scalar.activation(inverse[:], inverse[:], ACT.Abs_reciprocal_sqrt)
+            return inverse
+
+        def rms_norm(x, y):
+            inverse = inverse_spread(x, eps_rms)
+            for b in range(CB):
+                nc.vector.tensor_tensor(y[b], x[b], inverse[:], ALU.mult)
+
+        def layer_norm(x, y, gain, shift):
+            minus_mean_ps = channel_mean(x, minus_mean_w)
+            centred = scratch.tile([P, CB, CHUNK], F32, name="centred")
+            for b in range(CB):
+                nc.vector.tensor_tensor(centred[:, b, :], x[b], minus_mean_ps[:], ALU.add)
+            inverse = inverse_spread(blocks(centred), eps_ln)
+            for b in range(CB):
+                nc.vector.tensor_tensor(centred[:, b, :], centred[:, b, :], inverse[:], ALU.mult)
+                nc.vector.tensor_scalar(y[b], centred[:, b, :], column(gain, b), column(shift, b), ALU.mult, ALU.add)
 
         def project(w_sb, m, x):
-            product = products.tile([P, x[0].shape[1]], F32, name="product")
+            product = products.tile([P, CHUNK], F32, name="product")
             for kb in range(len(x)):
                 nc.tensor.matmul(
                     product[:], w_sb[:, kb, m * P : (m + 1) * P], x[kb], start=(kb == 0), stop=(kb == len(x) - 1)
                 )
             return product
 
-        def blocks(tile):
-            return [tile[:, b, :] for b in range(tile.shape[1])]
+        def blocks(tile, c0=0):
+            return [tile[:, b, c0 : c0 + CHUNK] for b in range(tile.shape[1])]
+
+        def operand(name):
+            return operands.tile([P, CB, CHUNK], BF16, name=name, tag="operand")
 
         e = held.tile([P, CB, S], BF16, name="e")
         table = [held.tile([P, S], F32, name=f"table{m}") for m in range(CB)]
-        for s0 in range(0, S, BANK):
-            e_piece = [e[:, b, s0 : s0 + BANK] for b in range(CB)]
-            normalise([emb_sb[:, b, s0 : s0 + BANK] for b in range(CB)], e_piece, EPS_RMS)
+        for s0 in range(0, S, CHUNK):
+            rms_norm(blocks(emb_sb, s0), blocks(e, s0))
+        u = {}
+        for t0 in chunks:
+            u[t0] = operand("u")
+            rms_norm(blocks(hidden_sb, t0), blocks(u[t0]))
+        for s0 in range(0, S, CHUNK):
             for m in range(CB):
-                nc.scalar.copy(table[m][:, s0 : s0 + BANK], project(w_fut_sb, m, e_piece)[:])
+                nc.scalar.copy(table[m][:, s0 : s0 + CHUNK], project(w_fut_sb, m, blocks(e, s0))[:])
 
-        def attention_block(t0):
-            u = work.tile([P, CB, CHUNK], BF16, name="u")
-            normalise([hidden_sb[:, b, t0 : t0 + CHUNK] for b in range(CB)], blocks(u), EPS_RMS)
-            q = work.tile([P, CB, CHUNK], F32, name="q")
-            curr = work.tile([P, CB, CHUNK], F32, name="curr")
+        x = {}
+        for t0 in chunks:
+            q = stream.tile([P, CB, CHUNK], F32, name="q")
+            x[t0] = stream.tile([P, CB, CHUNK], F32, name="x")
             piece = offsets[:, t0 // 16 : (t0 + CHUNK) // 16]
             for m in range(CB):
-                nc.scalar.activation(q[:, m, :], project(w_hid_sb, m, blocks(u))[:], ACT.Identity, bias=column("proj_b", m))
-                nc.vector.tensor_tensor(curr[:, m, :], table[m][:].indirect(piece), q[:, m, :], ALU.add)
-            xn = work.tile([P, CB, CHUNK], BF16, name="xn")
-            normalise(blocks(curr), blocks(xn), EPS_LN, "ln1_a", "ln1_b")
-            v = work.tile([P, CB, CHUNK], BF16, name="v")
+                nc.scalar.activation(
+                    q[:, m, :], project(w_hid_sb, m, blocks(u[t0]))[:], ACT.Identity, bias=column("proj_b", m)
+                )
+                nc.vector.tensor_tensor(x[t0][:, m, :], table[m][:].indirect(piece), q[:, m, :], ALU.add)
+
+        xn = {}
+        for t0 in chunks:
+            xn[t0] = operand("xn")
+            layer_norm(blocks(x[t0]), blocks(xn[t0]), "ln1_a", "ln1_b")
+        v = {}
+        for t0 in chunks:
+            v[t0] = operand("v")
             for m in range(CB):
-                nc.scalar.activation(v[:, m, :], project(w_v_sb, m, blocks(xn))[:], ACT.Identity, bias=column("b_v", m))
-            x1 = kept.tile([P, CB, CHUNK], F32, name="x1")
+                nc.scalar.activation(
+                    v[t0][:, m, :], project(w_v_sb, m, blocks(xn[t0]))[:], ACT.Identity, bias=column("b_v", m)
+                )
+        for t0 in chunks:
             for m in range(CB):
                 nc.vector.scalar_tensor_tensor(
-                    x1[:, m, :], project(w_o_sb, m, blocks(v))[:], column("b_o", m), curr[:, m, :], ALU.add, ALU.add
+                    x[t0][:, m, :], project(w_o_sb, m, blocks(v[t0]))[:], column("b_o", m), x[t0][:, m, :],
+                    ALU.add, ALU.add,
                 )
-            xn2 = kept.tile([P, CB, CHUNK], BF16, name="xn2")
-            normalise(blocks(x1), blocks(xn2), EPS_LN, "ln2_a", "ln2_b")
-            return x1, xn2
+        xn2 = {}
+        for t0 in chunks:
+            xn2[t0] = stream.tile([P, CB, CHUNK], BF16, name="xn2")
+            layer_norm(blocks(x[t0]), blocks(xn2[t0]), "ln2_a", "ln2_b")
 
-        def mlp_and_logits(t0, x1, xn2):
-            h = work.tile([P, FB, CHUNK], BF16, name="h")
+        for t0 in chunks:
+            h = wide.tile([P, FB, CHUNK], BF16, name="h")
             for f in range(FB):
                 nc.scalar.activation(
-                    h[:, f, :], project(fc_w_sb, f, blocks(xn2))[:], ACT.Gelu_apprx_tanh, bias=column("fc_b", f)
+                    h[:, f, :], project(fc_w_sb, f, blocks(xn2[t0]))[:], ACT.Gelu_apprx_tanh, bias=column("fc_b", f)
                 )
-            x2 = work.tile([P, CB, CHUNK], BF16, name="x2")
+            x2 = wide.tile([P, CB, CHUNK], BF16, name="x2")
             for m in range(CB):
                 nc.vector.scalar_tensor_tensor(
-                    x2[:, m, :], project(fcp_w_sb, m, blocks(h))[:], column("fcp_b", m), x1[:, m, :], ALU.add, ALU.add
+                    x2[:, m, :], project(fcp_w_sb, m, blocks(h))[:], column("fcp_b", m), x[t0][:, m, :],
+                    ALU.add, ALU.add,
                 )
             for t in range(SB):
                 logit = logits.tile([P, CHUNK], F32, name="logit")
-                nc.scalar.activation(
-                    logit[:], project(unembd_w_sb, t, blocks(x2))[:], ACT.Identity, bias=column("unembd_b", t)
-                )
+                nc.vector.tensor_scalar_add(logit[:], project(unembd_w_sb, t, blocks(x2))[:], column("unembd_b", t))
                 nc.sync.dma_start(out[t * P : (t + 1) * P, t0 : t0 + CHUNK], logit[:])
-
-        starts = list(range(0, N, CHUNK))
-        ready = {starts[0]: attention_block(starts[0])}
-        for t0 in starts:
-            if t0 + CHUNK < N:
-                ready[t0 + CHUNK] = attention_block(t0 + CHUNK)
-            x1, xn2 = ready[t0]
-            mlp_and_logits(t0, x1, xn2)

@@ -10,6 +10,7 @@ C, S, N, F = 384, 1024, 1536, 1536
 CB, SB, FB = C // P, S // P, F // P
 CHUNK = 512
 EPS_RMS, EPS_LN = 1e-8, 1e-6
+TINY = 1e-30
 
 FLOPS = 2 * (C * C * S + 3 * C * C * N + 2 * C * F * N + C * S * N)
 
@@ -27,8 +28,8 @@ def tile_mtp_b_kernel(
         tc.tile_pool(name="scratch", bufs=3) as scratch,
         tc.tile_pool(name="wide", bufs=2) as wide,
         tc.tile_pool(name="logits", bufs=4) as logits,
-        tc.psum_pool(name="means", bufs=2) as means,
-        tc.psum_pool(name="products", bufs=6) as products,
+        tc.psum_pool(name="means", bufs=3) as means,
+        tc.psum_pool(name="products", bufs=5) as products,
     ):
         offsets = held.tile([P, N // 16], U16, name="offsets")
         nc.sync.dma_start(offsets[:], offs)
@@ -47,6 +48,19 @@ def tile_mtp_b_kernel(
         for s0 in range(0, S, CHUNK):
             load_columns(emb_sb, emb, s0)
         w_fut_sb = load_weights(w_fut, "w_fut_sb")
+        vectors = {
+            "proj_b": proj_b, "ln1_a": ln1_a, "ln1_b": ln1_b, "b_v": b_v, "b_o": b_o, "ln2_a": ln2_a,
+            "ln2_b": ln2_b, "fcp_b": fcp_b, "fc_b": fc_b, "unembd_b": unembd_b,
+        }
+        first_row = {}
+        n_rows = 0
+        for name, vec in vectors.items():
+            first_row[name] = n_rows
+            n_rows += vec.shape[0] // P
+        rows = held.tile([n_rows, P], F32, name="rows")
+        for name, vec in vectors.items():
+            r0 = first_row[name]
+            nc.sync.dma_start(rows[r0 : r0 + vec.shape[0] // P, :], vec.rearrange("(b p) o -> b (p o)", p=P))
         for t0 in chunks:
             load_columns(hidden_sb, hidden, t0)
         w_hid_sb = load_weights(w_hid, "w_hid_sb")
@@ -64,65 +78,59 @@ def tile_mtp_b_kernel(
         nc.vector.memset(eps_rms[:], EPS_RMS)
         eps_ln = held.tile([P, 1], F32, name="eps_ln")
         nc.vector.memset(eps_ln[:], EPS_LN)
+        tiny = held.tile([P, 1], F32, name="tiny")
+        nc.vector.memset(tiny[:], TINY)
         ident = held.tile([P, P], F32, name="ident")
         masks.make_identity(nc, ident[:])
-
-        vectors = {
-            "proj_b": proj_b, "ln1_a": ln1_a, "ln1_b": ln1_b, "b_v": b_v, "b_o": b_o, "ln2_a": ln2_a,
-            "ln2_b": ln2_b, "fcp_b": fcp_b, "fc_b": fc_b, "unembd_b": unembd_b,
-        }
-        first_row = {}
-        n_rows = 0
-        for name, vec in vectors.items():
-            first_row[name] = n_rows
-            n_rows += vec.shape[0] // P
-        rows = held.tile([n_rows, P], F32, name="rows")
-        for name, vec in vectors.items():
-            r0 = first_row[name]
-            nc.scalar.dma_start(rows[r0 : r0 + vec.shape[0] // P, :], vec.rearrange("(b p) o -> b (p o)", p=P))
-        columns_ps = means.tile([P, n_rows], F32, tag="mean_ps")
-        nc.tensor.transpose(columns_ps[:], rows[:], ident[0:n_rows, 0:n_rows])
-        columns = held.tile([P, n_rows], F32, name="columns")
-        nc.vector.tensor_copy(columns[:], columns_ps[:])
 
         def column(name, block):
             c = first_row[name] + block
             return columns[:, c : c + 1]
 
-        def channel_mean(x, weights):
-            pair = scratch.tile([P, CHUNK], F32, name="pair")
-            nc.gpsimd.tensor_tensor(pair[:], x[0], x[1], ALU.add)
-            total = scratch.tile([P, CHUNK], F32, name="total")
-            nc.gpsimd.tensor_tensor(total[:], pair[:], x[2], ALU.add)
-            mean_ps = means.tile([P, CHUNK], F32, name="mean_ps")
-            nc.tensor.matmul(mean_ps[:], weights[:], total[:], start=True, stop=True)
-            return mean_ps
+        def channel_means(xs, weights):
+            pairs = [scratch.tile([P, CHUNK], F32, name="pair") for x in xs]
+            for x, pair in zip(xs, pairs):
+                nc.gpsimd.tensor_tensor(pair[:], x[0], x[1], ALU.add)
+            totals = [scratch.tile([P, CHUNK], F32, name="total") for x in xs]
+            for x, pair, total in zip(xs, pairs, totals):
+                nc.gpsimd.tensor_tensor(total[:], pair[:], x[2], ALU.add)
+            means_ps = [means.tile([P, CHUNK], F32, name="mean_ps") for x in xs]
+            for total, mean_ps in zip(totals, means_ps):
+                nc.tensor.matmul(mean_ps[:], weights[:], total[:], start=True, stop=True)
+            return means_ps
 
-        def inverse_spread(x, eps):
-            squares = scratch.tile([P, CB, CHUNK], F32, name="squares")
-            for b in range(CB):
-                nc.scalar.activation(squares[:, b, :], x[b], ACT.Square)
-            mean_ps = channel_mean(blocks(squares), mean_w)
-            inverse = scratch.tile([P, CHUNK], F32, name="inverse")
-            nc.scalar.activation(inverse[:], mean_ps[:], ACT.Sqrt)
-            nc.scalar.activation(inverse[:], inverse[:], ACT.Square, bias=eps[:])
-            nc.scalar.activation(inverse[:], inverse[:], ACT.Abs_reciprocal_sqrt)
-            return inverse
+        def inverse_spreads(xs, eps):
+            squares = [scratch.tile([P, CB, CHUNK], F32, name="squares") for x in xs]
+            for x, square in zip(xs, squares):
+                for b in range(CB):
+                    nc.scalar.activation(square[:, b, :], x[b], ACT.Square)
+            means_ps = channel_means([blocks(square) for square in squares], mean_w)
+            inverses = [scratch.tile([P, CHUNK], F32, name="inverse") for x in xs]
+            for mean_ps, inverse in zip(means_ps, inverses):
+                nc.scalar.activation(inverse[:], mean_ps[:], ACT.Abs_reciprocal_sqrt, bias=tiny[:])
+            for mean_ps, inverse in zip(means_ps, inverses):
+                nc.vector.tensor_tensor(inverse[:], mean_ps[:], inverse[:], ALU.mult)
+            for inverse in inverses:
+                nc.scalar.activation(inverse[:], inverse[:], ACT.Square, bias=eps[:])
+            for inverse in inverses:
+                nc.scalar.activation(inverse[:], inverse[:], ACT.Abs_reciprocal_sqrt)
+            return inverses
 
-        def rms_norm(x, y):
-            inverse = inverse_spread(x, eps_rms)
-            for b in range(CB):
-                nc.vector.tensor_tensor(y[b], x[b], inverse[:], ALU.mult)
+        def rms_norms(xs, ys):
+            for x, y, inverse in zip(xs, ys, inverse_spreads(xs, eps_rms)):
+                for b in range(CB):
+                    nc.vector.tensor_tensor(y[b], x[b], inverse[:], ALU.mult)
 
-        def layer_norm(x, y, gain, shift):
-            minus_mean_ps = channel_mean(x, minus_mean_w)
-            centred = scratch.tile([P, CB, CHUNK], F32, name="centred")
-            for b in range(CB):
-                nc.vector.tensor_tensor(centred[:, b, :], x[b], minus_mean_ps[:], ALU.add)
-            inverse = inverse_spread(blocks(centred), eps_ln)
-            for b in range(CB):
-                nc.vector.tensor_tensor(centred[:, b, :], centred[:, b, :], inverse[:], ALU.mult)
-                nc.vector.tensor_scalar(y[b], centred[:, b, :], column(gain, b), column(shift, b), ALU.mult, ALU.add)
+        def layer_norms(xs, ys, gain, shift):
+            centreds = [scratch.tile([P, CB, CHUNK], F32, name="centred") for x in xs]
+            for x, centred, minus_mean_ps in zip(xs, centreds, channel_means(xs, minus_mean_w)):
+                for b in range(CB):
+                    nc.vector.tensor_tensor(centred[:, b, :], x[b], minus_mean_ps[:], ALU.add)
+            inverses = inverse_spreads([blocks(centred) for centred in centreds], eps_ln)
+            for y, centred, inverse in zip(ys, centreds, inverses):
+                for b in range(CB):
+                    nc.vector.tensor_tensor(centred[:, b, :], centred[:, b, :], inverse[:], ALU.mult)
+                    nc.vector.tensor_scalar(y[b], centred[:, b, :], column(gain, b), column(shift, b), ALU.mult, ALU.add)
 
         def project(w_sb, m, x):
             product = products.tile([P, CHUNK], F32, name="product")
@@ -140,12 +148,13 @@ def tile_mtp_b_kernel(
 
         e = held.tile([P, CB, S], BF16, name="e")
         table = [held.tile([P, S], F32, name=f"table{m}") for m in range(CB)]
-        for s0 in range(0, S, CHUNK):
-            rms_norm(blocks(emb_sb, s0), blocks(e, s0))
-        u = {}
-        for t0 in chunks:
-            u[t0] = operand("u")
-            rms_norm(blocks(hidden_sb, t0), blocks(u[t0]))
+        rms_norms([blocks(emb_sb, s0) for s0 in range(0, S, CHUNK)], [blocks(e, s0) for s0 in range(0, S, CHUNK)])
+        u = {t0: operand("u") for t0 in chunks}
+        rms_norms([blocks(hidden_sb, t0) for t0 in chunks], [blocks(u[t0]) for t0 in chunks])
+        columns_ps = means.tile([P, n_rows], F32, tag="mean_ps")
+        nc.tensor.transpose(columns_ps[:], rows[:], ident[0:n_rows, 0:n_rows])
+        columns = held.tile([P, n_rows], F32, name="columns")
+        nc.vector.tensor_copy(columns[:], columns_ps[:])
         for s0 in range(0, S, CHUNK):
             for m in range(CB):
                 nc.scalar.copy(table[m][:, s0 : s0 + CHUNK], project(w_fut_sb, m, blocks(e, s0))[:])
@@ -161,10 +170,8 @@ def tile_mtp_b_kernel(
                 )
                 nc.vector.tensor_tensor(x[t0][:, m, :], table[m][:].indirect(piece), q[:, m, :], ALU.add)
 
-        xn = {}
-        for t0 in chunks:
-            xn[t0] = operand("xn")
-            layer_norm(blocks(x[t0]), blocks(xn[t0]), "ln1_a", "ln1_b")
+        xn = {t0: operand("xn") for t0 in chunks}
+        layer_norms([blocks(x[t0]) for t0 in chunks], [blocks(xn[t0]) for t0 in chunks], "ln1_a", "ln1_b")
         v = {}
         for t0 in chunks:
             v[t0] = operand("v")
@@ -178,24 +185,35 @@ def tile_mtp_b_kernel(
                     x[t0][:, m, :], project(w_o_sb, m, blocks(v[t0]))[:], column("b_o", m), x[t0][:, m, :],
                     ALU.add, ALU.add,
                 )
-        xn2 = {}
-        for t0 in chunks:
-            xn2[t0] = stream.tile([P, CB, CHUNK], BF16, name="xn2")
-            layer_norm(blocks(x[t0]), blocks(xn2[t0]), "ln2_a", "ln2_b")
+        xn2 = {t0: stream.tile([P, CB, CHUNK], BF16, name="xn2") for t0 in chunks}
+        layer_norms([blocks(x[t0]) for t0 in chunks], [blocks(xn2[t0]) for t0 in chunks], "ln2_a", "ln2_b")
 
-        for t0 in chunks:
+        def first_layer(t0):
             h = wide.tile([P, FB, CHUNK], BF16, name="h")
             for f in range(FB):
                 nc.scalar.activation(
                     h[:, f, :], project(fc_w_sb, f, blocks(xn2[t0]))[:], ACT.Gelu_apprx_tanh, bias=column("fc_b", f)
                 )
+            return h
+
+        def second_layer(t0, h):
             x2 = wide.tile([P, CB, CHUNK], BF16, name="x2")
             for m in range(CB):
                 nc.vector.scalar_tensor_tensor(
                     x2[:, m, :], project(fcp_w_sb, m, blocks(h))[:], column("fcp_b", m), x[t0][:, m, :],
                     ALU.add, ALU.add,
                 )
+            return x2
+
+        def unembed(t0, x2):
             for t in range(SB):
                 logit = logits.tile([P, CHUNK], F32, name="logit")
                 nc.vector.tensor_scalar_add(logit[:], project(unembd_w_sb, t, blocks(x2))[:], column("unembd_b", t))
                 nc.sync.dma_start(out[t * P : (t + 1) * P, t0 : t0 + CHUNK], logit[:])
+
+        h = first_layer(chunks[0])
+        for t0 in chunks:
+            x2 = second_layer(t0, h)
+            if t0 != chunks[-1]:
+                h = first_layer(t0 + CHUNK)
+            unembed(t0, x2)

@@ -88,12 +88,10 @@ def tile_mtp_b_kernel(
             return columns[:, c : c + 1]
 
         def channel_means(xs, weights):
-            pairs = [scratch.tile([P, CHUNK], F32, name="pair") for x in xs]
-            for x, pair in zip(xs, pairs):
-                nc.gpsimd.tensor_tensor(pair[:], x[0], x[1], ALU.add)
             totals = [scratch.tile([P, CHUNK], F32, name="total") for x in xs]
-            for x, pair, total in zip(xs, pairs, totals):
-                nc.gpsimd.tensor_tensor(total[:], pair[:], x[2], ALU.add)
+            for x, total in zip(xs, totals):
+                nc.vector.tensor_tensor(total[:], x[0], x[1], ALU.add)
+                nc.vector.tensor_tensor(total[:], total[:], x[2], ALU.add)
             means_ps = [means.tile([P, CHUNK], F32, name="mean_ps") for x in xs]
             for total, mean_ps in zip(totals, means_ps):
                 nc.tensor.matmul(mean_ps[:], weights[:], total[:], start=True, stop=True)
@@ -112,7 +110,6 @@ def tile_mtp_b_kernel(
                 nc.vector.tensor_tensor(inverse[:], mean_ps[:], inverse[:], ALU.mult)
             for inverse in inverses:
                 nc.scalar.activation(inverse[:], inverse[:], ACT.Square, bias=eps[:])
-            for inverse in inverses:
                 nc.scalar.activation(inverse[:], inverse[:], ACT.Abs_reciprocal_sqrt)
             return inverses
 
@@ -130,7 +127,7 @@ def tile_mtp_b_kernel(
             for y, centred, inverse in zip(ys, centreds, inverses):
                 for b in range(CB):
                     nc.vector.tensor_tensor(centred[:, b, :], centred[:, b, :], inverse[:], ALU.mult)
-                    nc.vector.tensor_scalar(y[b], centred[:, b, :], column(gain, b), column(shift, b), ALU.mult, ALU.add)
+                    nc.scalar.activation(y[b], centred[:, b, :], ACT.Identity, bias=column(shift, b), scale=column(gain, b))
 
         def project(w_sb, m, x):
             product = products.tile([P, CHUNK], F32, name="product")

@@ -9,6 +9,8 @@ P = 128
 C, S, N, F = 384, 1024, 1536, 1536
 CB, SB, FB = C // P, S // P, F // P
 CHUNK = 512
+JOB = 256
+PSUM_BANKS = 8
 EPS_RMS, EPS_LN = 1e-8, 1e-6
 TINY = 1e-30
 
@@ -21,15 +23,14 @@ def tile_mtp_b_kernel(
 ):
     nc = tc.nc
     chunks = list(range(0, N, CHUNK))
+    jobs = list(range(0, N, JOB))
+    first_group, second_group = jobs[: len(jobs) // 2], jobs[len(jobs) // 2 :]
     with (
         tc.tile_pool(name="held", bufs=1) as held,
-        tc.tile_pool(name="stream", bufs=len(chunks)) as stream,
-        tc.tile_pool(name="operands", bufs=len(chunks) + 1) as operands,
-        tc.tile_pool(name="scratch", bufs=3) as scratch,
+        tc.tile_pool(name="scratch", bufs=len(jobs)) as scratch,
         tc.tile_pool(name="wide", bufs=2) as wide,
         tc.tile_pool(name="logits", bufs=4) as logits,
-        tc.psum_pool(name="means", bufs=3) as means,
-        tc.psum_pool(name="products", bufs=5) as products,
+        tc.psum_pool(name="banks", bufs=PSUM_BANKS) as banks,
     ):
         offsets = held.tile([P, N // 16], U16, name="offsets")
         nc.sync.dma_start(offsets[:], offs)
@@ -83,134 +84,168 @@ def tile_mtp_b_kernel(
         ident = held.tile([P, P], F32, name="ident")
         masks.make_identity(nc, ident[:])
 
+        def bank(width, name):
+            return banks.tile([P, width], F32, name=name, tag="bank")
+
         def column(name, block):
             c = first_row[name] + block
             return columns[:, c : c + 1]
 
+        def blocks(tile, c0, width):
+            return [tile[:, b, c0 : c0 + width] for b in range(tile.shape[1])]
+
+        def nothing():
+            return None
+
         def channel_means(xs, weights):
-            totals = [scratch.tile([P, CHUNK], F32, name="total") for x in xs]
+            totals = [scratch.tile([P, JOB], F32, name="total") for x in xs]
             for x, total in zip(xs, totals):
                 nc.vector.tensor_tensor(total[:], x[0], x[1], ALU.add)
                 nc.vector.tensor_tensor(total[:], total[:], x[2], ALU.add)
-            means_ps = [means.tile([P, CHUNK], F32, name="mean_ps") for x in xs]
+            means_ps = [bank(JOB, "mean_ps") for x in xs]
             for total, mean_ps in zip(totals, means_ps):
                 nc.tensor.matmul(mean_ps[:], weights[:], total[:], start=True, stop=True)
             return means_ps
 
-        def inverse_spreads(xs, eps):
-            squares = [scratch.tile([P, CB, CHUNK], F32, name="squares") for x in xs]
-            for x, square in zip(xs, squares):
+        def norms(rms_jobs, layer_jobs, after_means=nothing, after_spreads=nothing):
+            def squares_of(x):
+                squares = scratch.tile([P, CB, JOB], F32, name="squares")
                 for b in range(CB):
-                    nc.scalar.activation(square[:, b, :], x[b], ACT.Square)
-            means_ps = channel_means([blocks(square) for square in squares], mean_w)
-            inverses = [scratch.tile([P, CHUNK], F32, name="inverse") for x in xs]
+                    nc.scalar.activation(squares[:, b, :], x[b], ACT.Square)
+                return blocks(squares, 0, JOB)
+
+            squared = [squares_of(x) for x, y in rms_jobs]
+            minus_means = channel_means([job[0] for job in layer_jobs], minus_mean_w)
+            after_means()
+            centreds = []
+            for job, minus_mean_ps in zip(layer_jobs, minus_means):
+                centred = scratch.tile([P, CB, JOB], F32, name="centred")
+                for b in range(CB):
+                    nc.vector.tensor_tensor(centred[:, b, :], job[0][b], minus_mean_ps[:], ALU.add)
+                centreds.append(blocks(centred, 0, JOB))
+                squared.append(squares_of(centreds[-1]))
+            means_ps = channel_means(squared, mean_w)
+            after_spreads()
+            epsilons = [eps_rms for job in rms_jobs] + [eps_ln for job in layer_jobs]
+            inverses = [scratch.tile([P, JOB], F32, name="inverse") for eps in epsilons]
             for mean_ps, inverse in zip(means_ps, inverses):
                 nc.scalar.activation(inverse[:], mean_ps[:], ACT.Abs_reciprocal_sqrt, bias=tiny[:])
             for mean_ps, inverse in zip(means_ps, inverses):
                 nc.vector.tensor_tensor(inverse[:], mean_ps[:], inverse[:], ALU.mult)
-            for inverse in inverses:
+            for eps, inverse in zip(epsilons, inverses):
                 nc.scalar.activation(inverse[:], inverse[:], ACT.Square, bias=eps[:])
                 nc.scalar.activation(inverse[:], inverse[:], ACT.Abs_reciprocal_sqrt)
-            return inverses
-
-        def rms_norms(xs, ys):
-            for x, y, inverse in zip(xs, ys, inverse_spreads(xs, eps_rms)):
+            for (x, y), inverse in zip(rms_jobs, inverses):
                 for b in range(CB):
                     nc.vector.tensor_tensor(y[b], x[b], inverse[:], ALU.mult)
-
-        def layer_norms(xs, ys, gain, shift):
-            centreds = [scratch.tile([P, CB, CHUNK], F32, name="centred") for x in xs]
-            for x, centred, minus_mean_ps in zip(xs, centreds, channel_means(xs, minus_mean_w)):
+            for (x, y, gain, shift), centred, inverse in zip(layer_jobs, centreds, inverses[len(rms_jobs) :]):
                 for b in range(CB):
-                    nc.vector.tensor_tensor(centred[:, b, :], x[b], minus_mean_ps[:], ALU.add)
-            inverses = inverse_spreads([blocks(centred) for centred in centreds], eps_ln)
-            for y, centred, inverse in zip(ys, centreds, inverses):
-                for b in range(CB):
-                    nc.vector.tensor_tensor(centred[:, b, :], centred[:, b, :], inverse[:], ALU.mult)
-                    nc.scalar.activation(y[b], centred[:, b, :], ACT.Identity, bias=column(shift, b), scale=column(gain, b))
+                    nc.vector.tensor_tensor(centred[b], centred[b], inverse[:], ALU.mult)
+                    nc.scalar.activation(y[b], centred[b], ACT.Identity, bias=column(shift, b), scale=column(gain, b))
 
         def project(w_sb, m, x):
-            product = products.tile([P, CHUNK], F32, name="product")
+            product = bank(x[0].shape[-1], "product")
             for kb in range(len(x)):
                 nc.tensor.matmul(
                     product[:], w_sb[:, kb, m * P : (m + 1) * P], x[kb], start=(kb == 0), stop=(kb == len(x) - 1)
                 )
             return product
 
-        def blocks(tile, c0=0):
-            return [tile[:, b, c0 : c0 + CHUNK] for b in range(tile.shape[1])]
-
-        def operand(name):
-            return operands.tile([P, CB, CHUNK], BF16, name=name, tag="operand")
-
         e = held.tile([P, CB, S], BF16, name="e")
         table = [held.tile([P, S], F32, name=f"table{m}") for m in range(CB)]
-        rms_norms([blocks(emb_sb, s0) for s0 in range(0, S, CHUNK)], [blocks(e, s0) for s0 in range(0, S, CHUNK)])
-        u = {t0: operand("u") for t0 in chunks}
-        rms_norms([blocks(hidden_sb, t0) for t0 in chunks], [blocks(u[t0]) for t0 in chunks])
-        columns_ps = means.tile([P, n_rows], F32, tag="mean_ps")
+        norms([(blocks(emb_sb, s0, JOB), blocks(e, s0, JOB)) for s0 in range(0, S, JOB)], [])
+        columns_ps = bank(n_rows, "columns_ps")
         nc.tensor.transpose(columns_ps[:], rows[:], ident[0:n_rows, 0:n_rows])
         columns = held.tile([P, n_rows], F32, name="columns")
         nc.vector.tensor_copy(columns[:], columns_ps[:])
         for s0 in range(0, S, CHUNK):
             for m in range(CB):
-                nc.scalar.copy(table[m][:, s0 : s0 + CHUNK], project(w_fut_sb, m, blocks(e, s0))[:])
+                nc.scalar.copy(table[m][:, s0 : s0 + CHUNK], project(w_fut_sb, m, blocks(e, s0, CHUNK))[:])
 
-        x = {}
-        for t0 in chunks:
-            q = stream.tile([P, CB, CHUNK], F32, name="q")
-            x[t0] = stream.tile([P, CB, CHUNK], F32, name="x")
-            piece = offsets[:, t0 // 16 : (t0 + CHUNK) // 16]
-            for m in range(CB):
-                nc.scalar.activation(
-                    q[:, m, :], project(w_hid_sb, m, blocks(u[t0]))[:], ACT.Identity, bias=column("proj_b", m)
-                )
-                nc.vector.tensor_tensor(x[t0][:, m, :], table[m][:].indirect(piece), q[:, m, :], ALU.add)
+        u = held.tile([P, CB, N], BF16, name="u")
+        x = held.tile([P, CB, N], F32, name="x")
+        xn = held.tile([P, CB, N], BF16, name="xn")
+        v = held.tile([P, CB, N], BF16, name="v")
+        xn2 = held.tile([P, CB, N], BF16, name="xn2")
 
-        xn = {t0: operand("xn") for t0 in chunks}
-        layer_norms([blocks(x[t0]) for t0 in chunks], [blocks(xn[t0]) for t0 in chunks], "ln1_a", "ln1_b")
-        v = {}
-        for t0 in chunks:
-            v[t0] = operand("v")
-            for m in range(CB):
-                nc.scalar.activation(
-                    v[t0][:, m, :], project(w_v_sb, m, blocks(xn[t0]))[:], ACT.Identity, bias=column("b_v", m)
-                )
-        for t0 in chunks:
-            for m in range(CB):
-                nc.vector.scalar_tensor_tensor(
-                    x[t0][:, m, :], project(w_o_sb, m, blocks(v[t0]))[:], column("b_o", m), x[t0][:, m, :],
-                    ALU.add, ALU.add,
-                )
-        xn2 = {t0: stream.tile([P, CB, CHUNK], BF16, name="xn2") for t0 in chunks}
-        layer_norms([blocks(x[t0]) for t0 in chunks], [blocks(xn2[t0]) for t0 in chunks], "ln2_a", "ln2_b")
+        def hidden_norms(group):
+            return [(blocks(hidden_sb, t0, JOB), blocks(u, t0, JOB)) for t0 in group]
+
+        def first_norms(group):
+            return [(blocks(x, t0, JOB), blocks(xn, t0, JOB), "ln1_a", "ln1_b") for t0 in group]
+
+        def second_norms(group):
+            return [(blocks(x, t0, JOB), blocks(xn2, t0, JOB), "ln2_a", "ln2_b") for t0 in group]
+
+        def look_up(group):
+            for t0 in group:
+                piece = offsets[:, t0 // 16 : (t0 + JOB) // 16]
+                for m in range(CB):
+                    q = scratch.tile([P, JOB], F32, name="q")
+                    nc.scalar.activation(
+                        q[:], project(w_hid_sb, m, blocks(u, t0, JOB))[:], ACT.Identity, bias=column("proj_b", m)
+                    )
+                    nc.vector.tensor_tensor(x[:, m, t0 : t0 + JOB], table[m][:].indirect(piece), q[:], ALU.add)
+
+        def values(group):
+            for t0 in group:
+                for m in range(CB):
+                    nc.scalar.activation(
+                        v[:, m, t0 : t0 + JOB], project(w_v_sb, m, blocks(xn, t0, JOB))[:], ACT.Identity,
+                        bias=column("b_v", m),
+                    )
+
+        def outputs(group):
+            for t0 in group:
+                for m in range(CB):
+                    x1 = x[:, m, t0 : t0 + JOB]
+                    nc.vector.scalar_tensor_tensor(
+                        x1, project(w_o_sb, m, blocks(v, t0, JOB))[:], column("b_o", m), x1, ALU.add, ALU.add
+                    )
 
         def first_layer(t0):
             h = wide.tile([P, FB, CHUNK], BF16, name="h")
             for f in range(FB):
                 nc.scalar.activation(
-                    h[:, f, :], project(fc_w_sb, f, blocks(xn2[t0]))[:], ACT.Gelu_apprx_tanh, bias=column("fc_b", f)
+                    h[:, f, :], project(fc_w_sb, f, blocks(xn2, t0, CHUNK))[:], ACT.Gelu_apprx_tanh,
+                    bias=column("fc_b", f),
                 )
             return h
 
-        def second_layer(t0, h):
-            x2 = wide.tile([P, CB, CHUNK], BF16, name="x2")
-            for m in range(CB):
+        def second_layer(t0, h, x2, some_blocks):
+            for m in some_blocks:
                 nc.vector.scalar_tensor_tensor(
-                    x2[:, m, :], project(fcp_w_sb, m, blocks(h))[:], column("fcp_b", m), x[t0][:, m, :],
-                    ALU.add, ALU.add,
+                    x2[:, m, :], project(fcp_w_sb, m, blocks(h, 0, CHUNK))[:], column("fcp_b", m),
+                    x[:, m, t0 : t0 + CHUNK], ALU.add, ALU.add,
                 )
-            return x2
 
-        def unembed(t0, x2):
-            for t in range(SB):
+        def unembed(t0, x2, some_blocks):
+            for t in some_blocks:
                 logit = logits.tile([P, CHUNK], F32, name="logit")
-                nc.vector.tensor_scalar_add(logit[:], project(unembd_w_sb, t, blocks(x2))[:], column("unembd_b", t))
+                nc.vector.tensor_scalar_add(
+                    logit[:], project(unembd_w_sb, t, blocks(x2, 0, CHUNK))[:], column("unembd_b", t)
+                )
                 nc.sync.dma_start(out[t * P : (t + 1) * P, t0 : t0 + CHUNK], logit[:])
 
+        norms(hidden_norms(first_group), [])
+        look_up(first_group)
+        norms(hidden_norms(second_group), [])
+        norms([], first_norms(first_group), lambda: look_up(second_group[:1]), lambda: look_up(second_group[1:]))
+        norms([], first_norms(second_group), lambda: values(first_group), lambda: outputs(first_group))
+        norms([], second_norms(first_group), lambda: values(second_group), lambda: outputs(second_group))
         h = first_layer(chunks[0])
-        for t0 in chunks:
-            x2 = second_layer(t0, h)
+        x2 = wide.tile([P, CB, CHUNK], BF16, name="x2")
+
+        def rest_of_second_layer():
+            second_layer(chunks[0], h, x2, [CB - 1])
+            unembed(chunks[0], x2, range(0, SB // 2))
+
+        norms([], second_norms(second_group), lambda: second_layer(chunks[0], h, x2, range(CB - 1)), rest_of_second_layer)
+        unembed(chunks[0], x2, range(SB // 2, SB))
+        h = first_layer(chunks[1])
+        for t0 in chunks[1:]:
+            x2 = wide.tile([P, CB, CHUNK], BF16, name="x2")
+            second_layer(t0, h, x2, range(CB))
             if t0 != chunks[-1]:
                 h = first_layer(t0 + CHUNK)
-            unembed(t0, x2)
+            unembed(t0, x2, range(SB))

@@ -10,6 +10,7 @@ C, S, N, F = 384, 1024, 1536, 1536
 CB, SB, FB = C // P, S // P, F // P
 CHUNK = 512
 JOB = 256
+TB = CHUNK // P
 PSUM_BANKS = 8
 EPS_RMS, EPS_LN = 1e-8, 1e-6
 TINY = 1e-30
@@ -23,11 +24,11 @@ def tile_mtp_b_kernel(
 ):
     nc = tc.nc
     chunks = list(range(0, N, CHUNK))
-    jobs = list(range(0, N, JOB))
-    first_group, second_group = jobs[: len(jobs) // 2], jobs[len(jobs) // 2 :]
     with (
         tc.tile_pool(name="held", bufs=1) as held,
-        tc.tile_pool(name="scratch", bufs=len(jobs)) as scratch,
+        tc.tile_pool(name="scratch", bufs=6) as scratch,
+        tc.tile_pool(name="flipped", bufs=2 * TB) as flipped,
+        tc.tile_pool(name="moments", bufs=4) as moments,
         tc.tile_pool(name="wide", bufs=2) as wide,
         tc.tile_pool(name="logits", bufs=4) as logits,
         tc.psum_pool(name="banks", bufs=PSUM_BANKS) as banks,
@@ -73,12 +74,8 @@ def tile_mtp_b_kernel(
 
         mean_w = held.tile([P, P], F32, name="mean_w")
         nc.vector.memset(mean_w[:], 1.0 / C)
-        minus_mean_w = held.tile([P, P], F32, name="minus_mean_w")
-        nc.vector.memset(minus_mean_w[:], -1.0 / C)
         eps_rms = held.tile([P, 1], F32, name="eps_rms")
         nc.vector.memset(eps_rms[:], EPS_RMS)
-        eps_ln = held.tile([P, 1], F32, name="eps_ln")
-        nc.vector.memset(eps_ln[:], EPS_LN)
         tiny = held.tile([P, 1], F32, name="tiny")
         nc.vector.memset(tiny[:], TINY)
         ident = held.tile([P, P], F32, name="ident")
@@ -94,66 +91,47 @@ def tile_mtp_b_kernel(
         def blocks(tile, c0, width):
             return [tile[:, b, c0 : c0 + width] for b in range(tile.shape[1])]
 
-        def nothing():
-            return None
-
-        def channel_means(xs, weights):
-            totals = [scratch.tile([P, JOB], F32, name="total") for x in xs]
-            for x, total in zip(xs, totals):
-                nc.vector.tensor_tensor(total[:], x[0], x[1], ALU.add)
-                nc.vector.tensor_tensor(total[:], total[:], x[2], ALU.add)
-            means_ps = [bank(JOB, "mean_ps") for x in xs]
+        def rms_norms(jobs):
+            squares = [scratch.tile([P, CB, JOB], F32, name="squares") for job in jobs]
+            for (x, y), square in zip(jobs, squares):
+                for b in range(CB):
+                    nc.scalar.activation(square[:, b, :], x[b], ACT.Square)
+            totals = [scratch.tile([P, JOB], F32, name="total") for job in jobs]
+            for square, total in zip(squares, totals):
+                nc.vector.tensor_tensor(total[:], square[:, 0, :], square[:, 1, :], ALU.add)
+                nc.vector.tensor_tensor(total[:], total[:], square[:, 2, :], ALU.add)
+            means_ps = [bank(JOB, "mean_ps") for job in jobs]
             for total, mean_ps in zip(totals, means_ps):
-                nc.tensor.matmul(mean_ps[:], weights[:], total[:], start=True, stop=True)
-            return means_ps
-
-        def norms(rms_jobs, layer_jobs, after_means=nothing, after_spreads=nothing):
-            def squares_of(x):
-                squares = scratch.tile([P, CB, JOB], F32, name="squares")
-                for b in range(CB):
-                    nc.scalar.activation(squares[:, b, :], x[b], ACT.Square)
-                return blocks(squares, 0, JOB)
-
-            squared = [squares_of(x) for x, y in rms_jobs]
-            minus_means = channel_means([job[0] for job in layer_jobs], minus_mean_w)
-            after_means()
-            centreds = []
-            for job, minus_mean_ps in zip(layer_jobs, minus_means):
-                centred = scratch.tile([P, CB, JOB], F32, name="centred")
-                for b in range(CB):
-                    nc.vector.tensor_tensor(centred[:, b, :], job[0][b], minus_mean_ps[:], ALU.add)
-                centreds.append(blocks(centred, 0, JOB))
-                squared.append(squares_of(centreds[-1]))
-            means_ps = channel_means(squared, mean_w)
-            after_spreads()
-            epsilons = [eps_rms for job in rms_jobs] + [eps_ln for job in layer_jobs]
-            inverses = [scratch.tile([P, JOB], F32, name="inverse") for eps in epsilons]
+                nc.tensor.matmul(mean_ps[:], mean_w[:], total[:], start=True, stop=True)
+            inverses = [scratch.tile([P, JOB], F32, name="inverse") for job in jobs]
             for mean_ps, inverse in zip(means_ps, inverses):
                 nc.scalar.activation(inverse[:], mean_ps[:], ACT.Abs_reciprocal_sqrt, bias=tiny[:])
             for mean_ps, inverse in zip(means_ps, inverses):
                 nc.vector.tensor_tensor(inverse[:], mean_ps[:], inverse[:], ALU.mult)
-            for eps, inverse in zip(epsilons, inverses):
-                nc.scalar.activation(inverse[:], inverse[:], ACT.Square, bias=eps[:])
+            for inverse in inverses:
+                nc.scalar.activation(inverse[:], inverse[:], ACT.Square, bias=eps_rms[:])
                 nc.scalar.activation(inverse[:], inverse[:], ACT.Abs_reciprocal_sqrt)
-            for (x, y), inverse in zip(rms_jobs, inverses):
+            for (x, y), inverse in zip(jobs, inverses):
                 for b in range(CB):
                     nc.vector.tensor_tensor(y[b], x[b], inverse[:], ALU.mult)
-            for (x, y, gain, shift), centred, inverse in zip(layer_jobs, centreds, inverses[len(rms_jobs) :]):
-                for b in range(CB):
-                    nc.vector.tensor_tensor(centred[b], centred[b], inverse[:], ALU.mult)
-                    nc.scalar.activation(y[b], centred[b], ACT.Identity, bias=column(shift, b), scale=column(gain, b))
 
-        def project(w_sb, m, x):
-            product = bank(x[0].shape[-1], "product")
-            for kb in range(len(x)):
+        def project(w_sb, m, operand):
+            product = bank(CHUNK, "product")
+            for kb in range(len(operand)):
                 nc.tensor.matmul(
-                    product[:], w_sb[:, kb, m * P : (m + 1) * P], x[kb], start=(kb == 0), stop=(kb == len(x) - 1)
+                    product[:], w_sb[:, kb, m * P : (m + 1) * P], operand[kb], start=(kb == 0),
+                    stop=(kb == len(operand) - 1),
                 )
             return product
 
         e = held.tile([P, CB, S], BF16, name="e")
+        u = held.tile([P, CB, N], BF16, name="u")
         table = [held.tile([P, S], F32, name=f"table{m}") for m in range(CB)]
-        norms([(blocks(emb_sb, s0, JOB), blocks(e, s0, JOB)) for s0 in range(0, S, JOB)], [])
+
+        def hidden_jobs(t0):
+            return [(blocks(hidden_sb, j0, JOB), blocks(u, j0, JOB)) for j0 in range(t0, t0 + CHUNK, JOB)]
+
+        rms_norms([(blocks(emb_sb, s0, JOB), blocks(e, s0, JOB)) for s0 in range(0, S, JOB)] + hidden_jobs(chunks[0]))
         columns_ps = bank(n_rows, "columns_ps")
         nc.tensor.transpose(columns_ps[:], rows[:], ident[0:n_rows, 0:n_rows])
         columns = held.tile([P, n_rows], F32, name="columns")
@@ -161,91 +139,114 @@ def tile_mtp_b_kernel(
         for s0 in range(0, S, CHUNK):
             for m in range(CB):
                 nc.scalar.copy(table[m][:, s0 : s0 + CHUNK], project(w_fut_sb, m, blocks(e, s0, CHUNK))[:])
+        rms_norms(hidden_jobs(chunks[1]) + hidden_jobs(chunks[2]))
 
-        u = held.tile([P, CB, N], BF16, name="u")
         x = held.tile([P, CB, N], F32, name="x")
         xn = held.tile([P, CB, N], BF16, name="xn")
         v = held.tile([P, CB, N], BF16, name="v")
         xn2 = held.tile([P, CB, N], BF16, name="xn2")
+        normals = {}
 
-        def hidden_norms(group):
-            return [(blocks(hidden_sb, t0, JOB), blocks(u, t0, JOB)) for t0 in group]
+        def look_up(t0):
+            piece = offsets[:, t0 // 16 : (t0 + CHUNK) // 16]
+            for m in range(CB):
+                q = scratch.tile([P, CHUNK], F32, name="q")
+                nc.scalar.activation(
+                    q[:], project(w_hid_sb, m, blocks(u, t0, CHUNK))[:], ACT.Identity, bias=column("proj_b", m)
+                )
+                nc.vector.tensor_tensor(x[:, m, t0 : t0 + CHUNK], table[m][:].indirect(piece), q[:], ALU.add)
 
-        def first_norms(group):
-            return [(blocks(x, t0, JOB), blocks(xn, t0, JOB), "ln1_a", "ln1_b") for t0 in group]
+        def normalise(t0):
+            tokens = []
+            for k in range(TB):
+                xt = bank(C, "xt")
+                for b in range(CB):
+                    nc.tensor.transpose(xt[:, b * P : (b + 1) * P], x[:, b, t0 + k * P : t0 + (k + 1) * P], ident[:])
+                tokens.append(xt)
+            mean_var = moments.tile([P, TB, 2], F32, name="mean_var")
+            for k in range(TB):
+                stats = moments.tile([P, 6], F32, name="stats")
+                nc.vector.bn_stats(stats[:], tokens[k][:])
+                nc.vector.bn_aggr(mean_var[:, k, :], stats[:])
+            mean, variance = mean_var[:, :, 0], mean_var[:, :, 1]
+            spread = moments.tile([P, TB], F32, name="spread")
+            nc.scalar.activation(spread[:], variance, ACT.Abs_reciprocal_sqrt, bias=tiny[:])
+            nc.vector.tensor_tensor(spread[:], spread[:], variance, ALU.mult)
+            nc.vector.tensor_scalar_add(spread[:], spread[:], EPS_LN)
+            inverse = moments.tile([P, TB], F32, name="inverse")
+            nc.vector.reciprocal(inverse[:], spread[:])
+            offset = moments.tile([P, TB], F32, name="offset")
+            nc.vector.scalar_tensor_tensor(offset[:], mean, -1.0, inverse[:], ALU.mult, ALU.mult)
+            normals[t0] = []
+            for k in range(TB):
+                normal = flipped.tile([P, C], F32, name="normal")
+                nc.scalar.activation(
+                    normal[:], tokens[k][:], ACT.Identity, bias=offset[:, k : k + 1], scale=inverse[:, k : k + 1]
+                )
+                normals[t0].append(normal)
 
-        def second_norms(group):
-            return [(blocks(x, t0, JOB), blocks(xn2, t0, JOB), "ln2_a", "ln2_b") for t0 in group]
+        def gain_and_shift(t0, y, gain, shift):
+            for b in range(CB):
+                channels = bank(CHUNK, "channels")
+                for k in range(TB):
+                    nc.tensor.transpose(channels[:, k * P : (k + 1) * P], normals[t0][k][:, b * P : (b + 1) * P], ident[:])
+                nc.scalar.activation(
+                    y[:, b, t0 : t0 + CHUNK], channels[:], ACT.Identity, bias=column(shift, b), scale=column(gain, b)
+                )
 
-        def look_up(group):
-            for t0 in group:
-                piece = offsets[:, t0 // 16 : (t0 + JOB) // 16]
-                for m in range(CB):
-                    q = scratch.tile([P, JOB], F32, name="q")
-                    nc.scalar.activation(
-                        q[:], project(w_hid_sb, m, blocks(u, t0, JOB))[:], ACT.Identity, bias=column("proj_b", m)
-                    )
-                    nc.vector.tensor_tensor(x[:, m, t0 : t0 + JOB], table[m][:].indirect(piece), q[:], ALU.add)
+        def values(t0):
+            for m in range(CB):
+                nc.scalar.activation(
+                    v[:, m, t0 : t0 + CHUNK], project(w_v_sb, m, blocks(xn, t0, CHUNK))[:], ACT.Identity,
+                    bias=column("b_v", m),
+                )
 
-        def values(group):
-            for t0 in group:
-                for m in range(CB):
-                    nc.scalar.activation(
-                        v[:, m, t0 : t0 + JOB], project(w_v_sb, m, blocks(xn, t0, JOB))[:], ACT.Identity,
-                        bias=column("b_v", m),
-                    )
+        def outputs(t0):
+            for m in range(CB):
+                x1 = x[:, m, t0 : t0 + CHUNK]
+                nc.vector.scalar_tensor_tensor(
+                    x1, project(w_o_sb, m, blocks(v, t0, CHUNK))[:], column("b_o", m), x1, ALU.add, ALU.add
+                )
 
-        def outputs(group):
-            for t0 in group:
-                for m in range(CB):
-                    x1 = x[:, m, t0 : t0 + JOB]
-                    nc.vector.scalar_tensor_tensor(
-                        x1, project(w_o_sb, m, blocks(v, t0, JOB))[:], column("b_o", m), x1, ALU.add, ALU.add
-                    )
+        hs, x2s = {}, {}
 
         def first_layer(t0):
-            h = wide.tile([P, FB, CHUNK], BF16, name="h")
+            hs[t0] = wide.tile([P, FB, CHUNK], BF16, name="h")
             for f in range(FB):
                 nc.scalar.activation(
-                    h[:, f, :], project(fc_w_sb, f, blocks(xn2, t0, CHUNK))[:], ACT.Gelu_apprx_tanh,
+                    hs[t0][:, f, :], project(fc_w_sb, f, blocks(xn2, t0, CHUNK))[:], ACT.Gelu_apprx_tanh,
                     bias=column("fc_b", f),
                 )
-            return h
 
-        def second_layer(t0, h, x2, some_blocks):
-            for m in some_blocks:
+        def second_layer(t0):
+            x2s[t0] = wide.tile([P, CB, CHUNK], BF16, name="x2")
+            for m in range(CB):
                 nc.vector.scalar_tensor_tensor(
-                    x2[:, m, :], project(fcp_w_sb, m, blocks(h, 0, CHUNK))[:], column("fcp_b", m),
+                    x2s[t0][:, m, :], project(fcp_w_sb, m, blocks(hs[t0], 0, CHUNK))[:], column("fcp_b", m),
                     x[:, m, t0 : t0 + CHUNK], ALU.add, ALU.add,
                 )
 
-        def unembed(t0, x2, some_blocks):
-            for t in some_blocks:
+        def unembed(t0):
+            for t in range(SB):
                 logit = logits.tile([P, CHUNK], F32, name="logit")
                 nc.vector.tensor_scalar_add(
-                    logit[:], project(unembd_w_sb, t, blocks(x2, 0, CHUNK))[:], column("unembd_b", t)
+                    logit[:], project(unembd_w_sb, t, blocks(x2s[t0], 0, CHUNK))[:], column("unembd_b", t)
                 )
                 nc.sync.dma_start(out[t * P : (t + 1) * P, t0 : t0 + CHUNK], logit[:])
 
-        norms(hidden_norms(first_group), [])
-        look_up(first_group)
-        norms(hidden_norms(second_group), [])
-        norms([], first_norms(first_group), lambda: look_up(second_group[:1]), lambda: look_up(second_group[1:]))
-        norms([], first_norms(second_group), lambda: values(first_group), lambda: outputs(first_group))
-        norms([], second_norms(first_group), lambda: values(second_group), lambda: outputs(second_group))
-        h = first_layer(chunks[0])
-        x2 = wide.tile([P, CB, CHUNK], BF16, name="x2")
-
-        def rest_of_second_layer():
-            second_layer(chunks[0], h, x2, [CB - 1])
-            unembed(chunks[0], x2, range(0, SB // 2))
-
-        norms([], second_norms(second_group), lambda: second_layer(chunks[0], h, x2, range(CB - 1)), rest_of_second_layer)
-        unembed(chunks[0], x2, range(SB // 2, SB))
-        h = first_layer(chunks[1])
-        for t0 in chunks[1:]:
-            x2 = wide.tile([P, CB, CHUNK], BF16, name="x2")
-            second_layer(t0, h, x2, range(CB))
-            if t0 != chunks[-1]:
-                h = first_layer(t0 + CHUNK)
-            unembed(t0, x2, range(SB))
+        stages = [
+            look_up,
+            normalise,
+            lambda t0: gain_and_shift(t0, xn, "ln1_a", "ln1_b"),
+            values,
+            outputs,
+            normalise,
+            lambda t0: gain_and_shift(t0, xn2, "ln2_a", "ln2_b"),
+            first_layer,
+            second_layer,
+            unembed,
+        ]
+        for step in range(len(stages) + len(chunks) - 1):
+            for i, t0 in enumerate(chunks):
+                if 0 <= step - i < len(stages):
+                    stages[step - i](t0)

@@ -9,11 +9,11 @@ P = 128
 C, S, N, F = 384, 1024, 1536, 1536
 CB, SB, FB = C // P, S // P, F // P
 CHUNK = 512
-JOB = 256
 TB = CHUNK // P
+PAIR = 2
 PSUM_BANKS = 8
 EPS_RMS, EPS_LN = 1e-8, 1e-6
-TINY = 1e-30
+TINY = 1e-26
 
 FLOPS = 2 * (C * C * S + 3 * C * C * N + 2 * C * F * N + C * S * N)
 
@@ -26,9 +26,10 @@ def tile_mtp_b_kernel(
     chunks = list(range(0, N, CHUNK))
     with (
         tc.tile_pool(name="held", bufs=1) as held,
-        tc.tile_pool(name="scratch", bufs=6) as scratch,
         tc.tile_pool(name="flipped", bufs=2 * TB) as flipped,
-        tc.tile_pool(name="moments", bufs=4) as moments,
+        tc.tile_pool(name="projected", bufs=CB) as projected,
+        tc.tile_pool(name="moments", bufs=8) as moments,
+        tc.tile_pool(name="unread", bufs=2) as unread,
         tc.tile_pool(name="wide", bufs=2) as wide,
         tc.tile_pool(name="logits", bufs=4) as logits,
         tc.psum_pool(name="banks", bufs=PSUM_BANKS) as banks,
@@ -60,9 +61,6 @@ def tile_mtp_b_kernel(
             first_row[name] = n_rows
             n_rows += vec.shape[0] // P
         rows = held.tile([n_rows, P], F32, name="rows")
-        for name, vec in vectors.items():
-            r0 = first_row[name]
-            nc.sync.dma_start(rows[r0 : r0 + vec.shape[0] // P, :], vec.rearrange("(b p) o -> b (p o)", p=P))
         for t0 in chunks:
             load_columns(hidden_sb, hidden, t0)
         w_hid_sb = load_weights(w_hid, "w_hid_sb")
@@ -72,14 +70,17 @@ def tile_mtp_b_kernel(
         fcp_w_sb = load_weights(fcp_w, "fcp_w_sb")
         unembd_w_sb = load_weights(unembd_w, "unembd_w_sb")
 
-        mean_w = held.tile([P, P], F32, name="mean_w")
-        nc.vector.memset(mean_w[:], 1.0 / C)
-        eps_rms = held.tile([P, 1], F32, name="eps_rms")
-        nc.vector.memset(eps_rms[:], EPS_RMS)
         tiny = held.tile([P, 1], F32, name="tiny")
         nc.vector.memset(tiny[:], TINY)
+        warm = held.tile([P, 1], F32, name="warm")
+        nc.scalar.activation(warm[:], tiny[:], ACT.Abs_reciprocal_sqrt)
         ident = held.tile([P, P], F32, name="ident")
         masks.make_identity(nc, ident[:])
+        ident_bf = held.tile([P, P], BF16, name="ident_bf")
+        masks.make_identity(nc, ident_bf[:])
+        for name, vec in vectors.items():
+            r0 = first_row[name]
+            nc.gpsimd.dma_start(rows[r0 : r0 + vec.shape[0] // P, :], vec.rearrange("(b p) o -> b (p o)", p=P))
 
         def bank(width, name):
             return banks.tile([P, width], F32, name=name, tag="bank")
@@ -90,30 +91,6 @@ def tile_mtp_b_kernel(
 
         def blocks(tile, c0, width):
             return [tile[:, b, c0 : c0 + width] for b in range(tile.shape[1])]
-
-        def rms_norms(jobs):
-            squares = [scratch.tile([P, CB, JOB], F32, name="squares") for job in jobs]
-            for (x, y), square in zip(jobs, squares):
-                for b in range(CB):
-                    nc.scalar.activation(square[:, b, :], x[b], ACT.Square)
-            totals = [scratch.tile([P, JOB], F32, name="total") for job in jobs]
-            for square, total in zip(squares, totals):
-                nc.vector.tensor_tensor(total[:], square[:, 0, :], square[:, 1, :], ALU.add)
-                nc.vector.tensor_tensor(total[:], total[:], square[:, 2, :], ALU.add)
-            means_ps = [bank(JOB, "mean_ps") for job in jobs]
-            for total, mean_ps in zip(totals, means_ps):
-                nc.tensor.matmul(mean_ps[:], mean_w[:], total[:], start=True, stop=True)
-            inverses = [scratch.tile([P, JOB], F32, name="inverse") for job in jobs]
-            for mean_ps, inverse in zip(means_ps, inverses):
-                nc.scalar.activation(inverse[:], mean_ps[:], ACT.Abs_reciprocal_sqrt, bias=tiny[:])
-            for mean_ps, inverse in zip(means_ps, inverses):
-                nc.vector.tensor_tensor(inverse[:], mean_ps[:], inverse[:], ALU.mult)
-            for inverse in inverses:
-                nc.scalar.activation(inverse[:], inverse[:], ACT.Square, bias=eps_rms[:])
-                nc.scalar.activation(inverse[:], inverse[:], ACT.Abs_reciprocal_sqrt)
-            for (x, y), inverse in zip(jobs, inverses):
-                for b in range(CB):
-                    nc.vector.tensor_tensor(y[b], x[b], inverse[:], ALU.mult)
 
         def project(w_sb, m, operand):
             product = bank(CHUNK, "product")
@@ -128,18 +105,16 @@ def tile_mtp_b_kernel(
         u = held.tile([P, CB, N], BF16, name="u")
         table = [held.tile([P, S], F32, name=f"table{m}") for m in range(CB)]
 
-        def hidden_jobs(t0):
-            return [(blocks(hidden_sb, j0, JOB), blocks(u, j0, JOB)) for j0 in range(t0, t0 + CHUNK, JOB)]
-
-        rms_norms([(blocks(emb_sb, s0, JOB), blocks(e, s0, JOB)) for s0 in range(0, S, JOB)] + hidden_jobs(chunks[0]))
-        columns_ps = bank(n_rows, "columns_ps")
-        nc.tensor.transpose(columns_ps[:], rows[:], ident[0:n_rows, 0:n_rows])
         columns = held.tile([P, n_rows], F32, name="columns")
-        nc.vector.tensor_copy(columns[:], columns_ps[:])
-        for s0 in range(0, S, CHUNK):
+
+        def turn_rows():
+            columns_ps = bank(n_rows, "columns_ps")
+            nc.tensor.transpose(columns_ps[:], rows[:], ident[0:n_rows, 0:n_rows])
+            nc.vector.tensor_copy(columns[:], columns_ps[:])
+
+        def project_table(s0):
             for m in range(CB):
                 nc.scalar.copy(table[m][:, s0 : s0 + CHUNK], project(w_fut_sb, m, blocks(e, s0, CHUNK))[:])
-        rms_norms(hidden_jobs(chunks[1]) + hidden_jobs(chunks[2]))
 
         x = held.tile([P, CB, N], F32, name="x")
         xn = held.tile([P, CB, N], BF16, name="xn")
@@ -150,48 +125,86 @@ def tile_mtp_b_kernel(
         def look_up(t0):
             piece = offsets[:, t0 // 16 : (t0 + CHUNK) // 16]
             for m in range(CB):
-                q = scratch.tile([P, CHUNK], F32, name="q")
+                q = projected.tile([P, CHUNK], F32, name="q")
                 nc.scalar.activation(
                     q[:], project(w_hid_sb, m, blocks(u, t0, CHUNK))[:], ACT.Identity, bias=column("proj_b", m)
                 )
                 nc.vector.tensor_tensor(x[:, m, t0 : t0 + CHUNK], table[m][:].indirect(piece), q[:], ALU.add)
 
-        def normalise(t0):
+        def flip(source, t0):
             tokens = []
             for k in range(TB):
                 xt = bank(C, "xt")
                 for b in range(CB):
-                    nc.tensor.transpose(xt[:, b * P : (b + 1) * P], x[:, b, t0 + k * P : t0 + (k + 1) * P], ident[:])
+                    nc.tensor.transpose(xt[:, b * P : (b + 1) * P], source[:, b, t0 + k * P : t0 + (k + 1) * P], ident[:])
                 tokens.append(xt)
-            mean_var = moments.tile([P, TB, 2], F32, name="mean_var")
-            for k in range(TB):
-                stats = moments.tile([P, 6], F32, name="stats")
-                nc.vector.bn_stats(stats[:], tokens[k][:])
-                nc.vector.bn_aggr(mean_var[:, k, :], stats[:])
-            mean, variance = mean_var[:, :, 0], mean_var[:, :, 1]
-            spread = moments.tile([P, TB], F32, name="spread")
-            nc.scalar.activation(spread[:], variance, ACT.Abs_reciprocal_sqrt, bias=tiny[:])
-            nc.vector.tensor_tensor(spread[:], spread[:], variance, ALU.mult)
-            nc.vector.tensor_scalar_add(spread[:], spread[:], EPS_LN)
-            inverse = moments.tile([P, TB], F32, name="inverse")
-            nc.vector.reciprocal(inverse[:], spread[:])
-            offset = moments.tile([P, TB], F32, name="offset")
-            nc.vector.scalar_tensor_tensor(offset[:], mean, -1.0, inverse[:], ALU.mult, ALU.mult)
+            return tokens
+
+        def inverse_spread(squares, scale, eps):
+            root = moments.tile([P, squares.shape[-1]], F32, name="root")
+            nc.scalar.activation(root[:], squares, ACT.Abs_reciprocal_sqrt, bias=tiny[:], scale=scale)
+            nc.vector.scalar_tensor_tensor(root[:], squares, scale, root[:], ALU.mult, ALU.mult)
+            nc.vector.tensor_scalar_add(root[:], root[:], eps)
+            inverse = moments.tile([P, squares.shape[-1]], F32, name="inverse")
+            nc.vector.reciprocal(inverse[:], root[:])
+            return inverse
+
+        def rms_normalise(source, t0):
+            tokens = flip(source, t0)
             normals[t0] = []
+            for k0 in range(0, TB, PAIR):
+                sums = moments.tile([P, PAIR], F32, name="sums")
+                for j in range(PAIR):
+                    junk = unread.tile([P, C], BF16, name="junk")
+                    nc.scalar.activation(junk[:], tokens[k0 + j][:], ACT.Square, accum_out=sums[:, j : j + 1])
+                inverse = inverse_spread(sums[:], 1.0 / C, EPS_RMS)
+                by_vector = flipped.tile([P, C], BF16, name="rms_normal")
+                nc.vector.tensor_scalar_mul(by_vector[:], tokens[k0][:], inverse[:, 0:1])
+                by_scalar = flipped.tile([P, C], BF16, name="rms_normal")
+                nc.scalar.activation(by_scalar[:], tokens[k0 + 1][:], ACT.Identity, scale=inverse[:, 1:2])
+                normals[t0].extend([by_vector, by_scalar])
+
+        def rms_back(t0, y):
+            channels = [banks.tile([P, CHUNK], BF16, name="rms_channels", tag="bank") for b in range(CB)]
             for k in range(TB):
-                normal = flipped.tile([P, C], F32, name="normal")
-                nc.scalar.activation(
-                    normal[:], tokens[k][:], ACT.Identity, bias=offset[:, k : k + 1], scale=inverse[:, k : k + 1]
+                for b in range(CB):
+                    nc.tensor.transpose(channels[b][:, k * P : (k + 1) * P], normals[t0][k][:, b * P : (b + 1) * P], ident_bf[:])
+            for b in range(CB):
+                nc.vector.tensor_copy(y[:, b, t0 : t0 + CHUNK], channels[b][:])
+
+        def normalise(t0):
+            tokens = flip(x, t0)
+            normals[t0] = []
+            for k0 in range(0, TB, PAIR):
+                mean_var = moments.tile([P, PAIR, 2], F32, name="mean_var")
+                for j in range(PAIR):
+                    stats = moments.tile([P, 6], F32, name="stats")
+                    nc.vector.bn_stats(stats[:], tokens[k0 + j][:])
+                    nc.vector.bn_aggr(mean_var[:, j, :], stats[:])
+                mean, variance = mean_var[:, :, 0], mean_var[:, :, 1]
+                inverse = inverse_spread(variance, 1.0, EPS_LN)
+                by_vector = flipped.tile([P, C], F32, name="normal")
+                nc.vector.tensor_scalar(
+                    by_vector[:], tokens[k0][:], mean_var[:, 0, 0:1], inverse[:, 0:1], ALU.subtract, ALU.mult
                 )
-                normals[t0].append(normal)
+                offset = moments.tile([P, PAIR], F32, name="offset")
+                nc.vector.scalar_tensor_tensor(offset[:], mean, -1.0, inverse[:], ALU.mult, ALU.mult)
+                by_scalar = flipped.tile([P, C], F32, name="normal")
+                nc.scalar.activation(
+                    by_scalar[:], tokens[k0 + 1][:], ACT.Identity, bias=offset[:, 1:2], scale=inverse[:, 1:2]
+                )
+                normals[t0].extend([by_vector, by_scalar])
 
         def gain_and_shift(t0, y, gain, shift):
+            channels = [bank(CHUNK, "channels") for b in range(CB)]
+            for k in range(TB):
+                for b in range(CB):
+                    nc.tensor.transpose(
+                        channels[b][:, k * P : (k + 1) * P], normals[t0][k][:, b * P : (b + 1) * P], ident[:]
+                    )
             for b in range(CB):
-                channels = bank(CHUNK, "channels")
-                for k in range(TB):
-                    nc.tensor.transpose(channels[:, k * P : (k + 1) * P], normals[t0][k][:, b * P : (b + 1) * P], ident[:])
                 nc.scalar.activation(
-                    y[:, b, t0 : t0 + CHUNK], channels[:], ACT.Identity, bias=column(shift, b), scale=column(gain, b)
+                    y[:, b, t0 : t0 + CHUNK], channels[b][:], ACT.Identity, bias=column(shift, b), scale=column(gain, b)
                 )
 
         def values(t0):
@@ -234,7 +247,14 @@ def tile_mtp_b_kernel(
                 )
                 nc.sync.dma_start(out[t * P : (t + 1) * P, t0 : t0 + CHUNK], logit[:])
 
-        stages = [
+        embedding_stages = [
+            lambda s0: rms_normalise(emb_sb, s0),
+            lambda s0: rms_back(s0, e),
+            project_table,
+        ]
+        token_stages = [
+            lambda t0: rms_normalise(hidden_sb, t0),
+            lambda t0: rms_back(t0, u),
             look_up,
             normalise,
             lambda t0: gain_and_shift(t0, xn, "ln1_a", "ln1_b"),
@@ -246,7 +266,11 @@ def tile_mtp_b_kernel(
             second_layer,
             unembed,
         ]
-        for step in range(len(stages) + len(chunks) - 1):
-            for i, t0 in enumerate(chunks):
+        lanes = [(embedding_stages, s0) for s0 in range(0, S, CHUNK)] + [(token_stages, t0) for t0 in chunks]
+        first_use_of_columns = len(lanes) - len(chunks) + token_stages.index(look_up)
+        for step in range(len(token_stages) + len(lanes) - 1):
+            if step == first_use_of_columns:
+                turn_rows()
+            for i, (stages, c0) in enumerate(lanes):
                 if 0 <= step - i < len(stages):
-                    stages[step - i](t0)
+                    stages[step - i](c0)

@@ -76,8 +76,6 @@ def tile_mtp_b_kernel(
         nc.scalar.activation(warm[:], tiny[:], ACT.Abs_reciprocal_sqrt)
         ident = held.tile([P, P], F32, name="ident")
         masks.make_identity(nc, ident[:])
-        ident_bf = held.tile([P, P], BF16, name="ident_bf")
-        masks.make_identity(nc, ident_bf[:])
         for name, vec in vectors.items():
             r0 = first_row[name]
             nc.gpsimd.dma_start(rows[r0 : r0 + vec.shape[0] // P, :], vec.rearrange("(b p) o -> b (p o)", p=P))
@@ -121,6 +119,7 @@ def tile_mtp_b_kernel(
         v = held.tile([P, CB, N], BF16, name="v")
         xn2 = held.tile([P, CB, N], BF16, name="xn2")
         normals = {}
+        inverses = {}
 
         def look_up(t0):
             piece = offsets[:, t0 // 16 : (t0 + CHUNK) // 16]
@@ -149,28 +148,23 @@ def tile_mtp_b_kernel(
             nc.vector.reciprocal(inverse[:], root[:])
             return inverse
 
-        def rms_normalise(source, t0):
+        def rms_count(source, t0):
             tokens = flip(source, t0)
-            normals[t0] = []
+            inverses[t0] = []
             for k0 in range(0, TB, PAIR):
                 sums = moments.tile([P, PAIR], F32, name="sums")
                 for j in range(PAIR):
                     junk = unread.tile([P, C], BF16, name="junk")
                     nc.scalar.activation(junk[:], tokens[k0 + j][:], ACT.Square, accum_out=sums[:, j : j + 1])
-                inverse = inverse_spread(sums[:], 1.0 / C, EPS_RMS)
-                by_vector = flipped.tile([P, C], BF16, name="rms_normal")
-                nc.vector.tensor_scalar_mul(by_vector[:], tokens[k0][:], inverse[:, 0:1])
-                by_scalar = flipped.tile([P, C], BF16, name="rms_normal")
-                nc.scalar.activation(by_scalar[:], tokens[k0 + 1][:], ACT.Identity, scale=inverse[:, 1:2])
-                normals[t0].extend([by_vector, by_scalar])
+                inverses[t0].append(inverse_spread(sums[:], 1.0 / C, EPS_RMS))
 
-        def rms_back(t0, y):
-            channels = [banks.tile([P, CHUNK], BF16, name="rms_channels", tag="bank") for b in range(CB)]
+        def rms_apply(source, t0, y):
+            spread = bank(CHUNK, "spread")
             for k in range(TB):
-                for b in range(CB):
-                    nc.tensor.transpose(channels[b][:, k * P : (k + 1) * P], normals[t0][k][:, b * P : (b + 1) * P], ident_bf[:])
+                inverse = inverses[t0][k // PAIR][:, k % PAIR : k % PAIR + 1]
+                nc.tensor.transpose(spread[:, k * P : (k + 1) * P], inverse.to_broadcast([P, P]), ident[:])
             for b in range(CB):
-                nc.vector.tensor_copy(y[:, b, t0 : t0 + CHUNK], channels[b][:])
+                nc.vector.tensor_tensor(y[:, b, t0 : t0 + CHUNK], source[:, b, t0 : t0 + CHUNK], spread[:], ALU.mult)
 
         def normalise(t0):
             tokens = flip(x, t0)
@@ -248,13 +242,13 @@ def tile_mtp_b_kernel(
                 nc.sync.dma_start(out[t * P : (t + 1) * P, t0 : t0 + CHUNK], logit[:])
 
         embedding_stages = [
-            lambda s0: rms_normalise(emb_sb, s0),
-            lambda s0: rms_back(s0, e),
+            lambda s0: rms_count(emb_sb, s0),
+            lambda s0: rms_apply(emb_sb, s0, e),
             project_table,
         ]
         token_stages = [
-            lambda t0: rms_normalise(hidden_sb, t0),
-            lambda t0: rms_back(t0, u),
+            lambda t0: rms_count(hidden_sb, t0),
+            lambda t0: rms_apply(hidden_sb, t0, u),
             look_up,
             normalise,
             lambda t0: gain_and_shift(t0, xn, "ln1_a", "ln1_b"),

@@ -13,7 +13,6 @@ TB = CHUNK // P
 PAIR = 2
 PSUM_BANKS = 8
 EPS_RMS, EPS_LN = 1e-8, 1e-6
-TINY = 1e-26
 
 FLOPS = 2 * (C * C * S + 3 * C * C * N + 2 * C * F * N + C * S * N)
 
@@ -52,7 +51,7 @@ def tile_mtp_b_kernel(
             load_columns(emb_sb, emb, s0)
         w_fut_sb = load_weights(w_fut, "w_fut_sb")
         vectors = {
-            "proj_b": proj_b, "ln1_a": ln1_a, "ln1_b": ln1_b, "b_v": b_v, "b_o": b_o, "ln2_a": ln2_a,
+            "ln1_a": ln1_a, "ln1_b": ln1_b, "b_v": b_v, "b_o": b_o, "ln2_a": ln2_a,
             "ln2_b": ln2_b, "fcp_b": fcp_b, "fc_b": fc_b, "unembd_b": unembd_b,
         }
         first_row = {}
@@ -61,6 +60,7 @@ def tile_mtp_b_kernel(
             first_row[name] = n_rows
             n_rows += vec.shape[0] // P
         rows = held.tile([n_rows, P], F32, name="rows")
+        proj_b_sb = held.tile([P, CB], F32, name="proj_b_sb")
         for t0 in chunks:
             load_columns(hidden_sb, hidden, t0)
         w_hid_sb = load_weights(w_hid, "w_hid_sb")
@@ -70,12 +70,12 @@ def tile_mtp_b_kernel(
         fcp_w_sb = load_weights(fcp_w, "fcp_w_sb")
         unembd_w_sb = load_weights(unembd_w, "unembd_w_sb")
 
-        tiny = held.tile([P, 1], F32, name="tiny")
-        nc.vector.memset(tiny[:], TINY)
         warm = held.tile([P, 1], F32, name="warm")
-        nc.scalar.activation(warm[:], tiny[:], ACT.Abs_reciprocal_sqrt)
+        nc.vector.memset(warm[:], 1.0)
+        nc.scalar.activation(warm[:], warm[:], ACT.Sqrt)
         ident = held.tile([P, P], F32, name="ident")
         masks.make_identity(nc, ident[:])
+        nc.gpsimd.dma_start(proj_b_sb[:], proj_b.rearrange("(b p) o -> p (b o)", p=P))
         for name, vec in vectors.items():
             r0 = first_row[name]
             nc.gpsimd.dma_start(rows[r0 : r0 + vec.shape[0] // P, :], vec.rearrange("(b p) o -> b (p o)", p=P))
@@ -108,7 +108,7 @@ def tile_mtp_b_kernel(
         def turn_rows():
             columns_ps = bank(n_rows, "columns_ps")
             nc.tensor.transpose(columns_ps[:], rows[:], ident[0:n_rows, 0:n_rows])
-            nc.vector.tensor_copy(columns[:], columns_ps[:])
+            nc.scalar.copy(columns[:], columns_ps[:])
 
         def project_table(s0):
             for m in range(CB):
@@ -122,13 +122,19 @@ def tile_mtp_b_kernel(
         inverses = {}
 
         def look_up(t0):
-            piece = offsets[:, t0 // 16 : (t0 + CHUNK) // 16]
+            qs = []
             for m in range(CB):
                 q = projected.tile([P, CHUNK], F32, name="q")
                 nc.scalar.activation(
-                    q[:], project(w_hid_sb, m, blocks(u, t0, CHUNK))[:], ACT.Identity, bias=column("proj_b", m)
+                    q[:], project(w_hid_sb, m, blocks(u, t0, CHUNK))[:], ACT.Identity, bias=proj_b_sb[:, m : m + 1]
                 )
-                nc.vector.tensor_tensor(x[:, m, t0 : t0 + CHUNK], table[m][:].indirect(piece), q[:], ALU.add)
+                qs.append(q)
+            for c in range(0, CHUNK, PAIR * P):
+                piece = offsets[:, (t0 + c) // 16 : (t0 + c + PAIR * P) // 16]
+                for m in range(CB):
+                    nc.vector.tensor_tensor(
+                        x[:, m, t0 + c : t0 + c + PAIR * P], table[m][:].indirect(piece), qs[m][:, c : c + PAIR * P], ALU.add
+                    )
 
         def flip(source, t0):
             tokens = []
@@ -141,8 +147,7 @@ def tile_mtp_b_kernel(
 
         def inverse_spread(squares, scale, eps):
             root = moments.tile([P, squares.shape[-1]], F32, name="root")
-            nc.scalar.activation(root[:], squares, ACT.Abs_reciprocal_sqrt, bias=tiny[:], scale=scale)
-            nc.vector.scalar_tensor_tensor(root[:], squares, scale, root[:], ALU.mult, ALU.mult)
+            nc.scalar.activation(root[:], squares, ACT.Sqrt, scale=scale)
             nc.vector.tensor_scalar_add(root[:], root[:], eps)
             inverse = moments.tile([P, squares.shape[-1]], F32, name="inverse")
             nc.vector.reciprocal(inverse[:], root[:])
@@ -260,11 +265,12 @@ def tile_mtp_b_kernel(
             second_layer,
             unembed,
         ]
-        lanes = [(embedding_stages, s0) for s0 in range(0, S, CHUNK)] + [(token_stages, t0) for t0 in chunks]
-        first_use_of_columns = len(lanes) - len(chunks) + token_stages.index(look_up)
-        for step in range(len(token_stages) + len(lanes) - 1):
-            if step == first_use_of_columns:
+        lanes = [(embedding_stages, 0, 0), (embedding_stages, CHUNK, 1)]
+        lanes += [(token_stages, t0, 1 + i) for i, t0 in enumerate(chunks)]
+        first_normalise = 1 + token_stages.index(normalise)
+        for step in range(lanes[-1][2] + len(token_stages)):
+            if step == first_normalise:
                 turn_rows()
-            for i, (stages, c0) in enumerate(lanes):
-                if 0 <= step - i < len(stages):
-                    stages[step - i](c0)
+            for stages, c0, first_step in lanes:
+                if 0 <= step - first_step < len(stages):
+                    stages[step - first_step](c0)

import concourse.masks as masks
import concourse.mybir as mybir

F32, BF16, U16 = mybir.dt.float32, mybir.dt.bfloat16, mybir.dt.uint16
ALU = mybir.AluOpType
ACT = mybir.ActivationFunctionType

P = 128
C, S, N, F = 384, 1024, 1536, 1536
CB, SB, FB = C // P, S // P, F // P
CHUNK = 512
TB = CHUNK // P
PAIR = 2
PSUM_BANKS = 8
EPS_RMS, EPS_LN = 1e-8, 1e-6

FLOPS = 2 * (C * C * S + 3 * C * C * N + 2 * C * F * N + C * S * N)


def tile_mtp_b_kernel(
    tc, emb, hidden, w_fut, w_hid, proj_b, ln1_a, ln1_b, w_v, b_v, w_o, b_o,
    ln2_a, ln2_b, fc_w, fc_b, fcp_w, fcp_b, unembd_w, unembd_b, offs, out,
):
    nc = tc.nc
    chunks = list(range(0, N, CHUNK))
    with (
        tc.tile_pool(name="held", bufs=1) as held,
        tc.tile_pool(name="flipped", bufs=2 * TB) as flipped,
        tc.tile_pool(name="projected", bufs=CB) as projected,
        tc.tile_pool(name="moments", bufs=8) as moments,
        tc.tile_pool(name="unread", bufs=2) as unread,
        tc.tile_pool(name="wide", bufs=2) as wide,
        tc.tile_pool(name="logits", bufs=4) as logits,
        tc.psum_pool(name="banks", bufs=PSUM_BANKS) as banks,
    ):
        offsets = held.tile([P, N // 16], U16, name="offsets")
        nc.sync.dma_start(offsets[:], offs)

        def load_columns(tile, source, c0):
            for b in range(CB):
                nc.sync.dma_start(tile[:, b, c0 : c0 + CHUNK], source[b * P : (b + 1) * P, c0 : c0 + CHUNK])

        def load_weights(w, name):
            tile = held.tile([P, w.shape[0] // P, w.shape[1]], BF16, name=name)
            nc.sync.dma_start(tile[:], w.rearrange("(kb p) m -> p kb m", p=P))
            return tile

        emb_sb = held.tile([P, CB, S], F32, name="emb_sb")
        hidden_sb = held.tile([P, CB, N], F32, name="hidden_sb")
        for s0 in range(0, S, CHUNK):
            load_columns(emb_sb, emb, s0)
        w_fut_sb = load_weights(w_fut, "w_fut_sb")
        vectors = {
            "ln1_a": ln1_a, "ln1_b": ln1_b, "b_v": b_v, "b_o": b_o, "ln2_a": ln2_a,
            "ln2_b": ln2_b, "fcp_b": fcp_b, "fc_b": fc_b, "unembd_b": unembd_b,
        }
        first_row = {}
        n_rows = 0
        for name, vec in vectors.items():
            first_row[name] = n_rows
            n_rows += vec.shape[0] // P
        rows = held.tile([n_rows, P], F32, name="rows")
        proj_b_sb = held.tile([P, CB], F32, name="proj_b_sb")
        for t0 in chunks:
            load_columns(hidden_sb, hidden, t0)
        w_hid_sb = load_weights(w_hid, "w_hid_sb")
        w_v_sb = load_weights(w_v, "w_v_sb")
        w_o_sb = load_weights(w_o, "w_o_sb")
        fc_w_sb = load_weights(fc_w, "fc_w_sb")
        fcp_w_sb = load_weights(fcp_w, "fcp_w_sb")
        unembd_w_sb = load_weights(unembd_w, "unembd_w_sb")

        warm = held.tile([P, 1], F32, name="warm")
        nc.vector.memset(warm[:], 1.0)
        nc.scalar.activation(warm[:], warm[:], ACT.Sqrt)
        ident = held.tile([P, P], F32, name="ident")
        masks.make_identity(nc, ident[:])
        nc.gpsimd.dma_start(proj_b_sb[:], proj_b.rearrange("(b p) o -> p (b o)", p=P))
        for name, vec in vectors.items():
            r0 = first_row[name]
            nc.gpsimd.dma_start(rows[r0 : r0 + vec.shape[0] // P, :], vec.rearrange("(b p) o -> b (p o)", p=P))

        def bank(width, name):
            return banks.tile([P, width], F32, name=name, tag="bank")

        def column(name, block):
            c = first_row[name] + block
            return columns[:, c : c + 1]

        def blocks(tile, c0, width):
            return [tile[:, b, c0 : c0 + width] for b in range(tile.shape[1])]

        def project(w_sb, m, operand):
            product = bank(CHUNK, "product")
            for kb in range(len(operand)):
                nc.tensor.matmul(
                    product[:], w_sb[:, kb, m * P : (m + 1) * P], operand[kb], start=(kb == 0),
                    stop=(kb == len(operand) - 1),
                )
            return product

        e = held.tile([P, CB, S], BF16, name="e")
        u = held.tile([P, CB, N], BF16, name="u")
        table = [held.tile([P, S], F32, name=f"table{m}") for m in range(CB)]

        columns = held.tile([P, n_rows], F32, name="columns")

        def turn_rows():
            columns_ps = bank(n_rows, "columns_ps")
            nc.tensor.transpose(columns_ps[:], rows[:], ident[0:n_rows, 0:n_rows])
            nc.scalar.copy(columns[:], columns_ps[:])

        def project_table(s0):
            for m in range(CB):
                nc.scalar.copy(table[m][:, s0 : s0 + CHUNK], project(w_fut_sb, m, blocks(e, s0, CHUNK))[:])

        x = held.tile([P, CB, N], F32, name="x")
        xn = held.tile([P, CB, N], BF16, name="xn")
        v = held.tile([P, CB, N], BF16, name="v")
        xn2 = held.tile([P, CB, N], BF16, name="xn2")
        normals = {}
        inverses = {}

        def look_up(t0):
            qs = []
            for m in range(CB):
                q = projected.tile([P, CHUNK], F32, name="q")
                nc.scalar.activation(
                    q[:], project(w_hid_sb, m, blocks(u, t0, CHUNK))[:], ACT.Identity, bias=proj_b_sb[:, m : m + 1]
                )
                qs.append(q)
            for c in range(0, CHUNK, PAIR * P):
                piece = offsets[:, (t0 + c) // 16 : (t0 + c + PAIR * P) // 16]
                for m in range(CB):
                    nc.vector.tensor_tensor(
                        x[:, m, t0 + c : t0 + c + PAIR * P], table[m][:].indirect(piece), qs[m][:, c : c + PAIR * P], ALU.add
                    )

        def flip(source, t0):
            tokens = []
            for k in range(TB):
                xt = bank(C, "xt")
                for b in range(CB):
                    nc.tensor.transpose(xt[:, b * P : (b + 1) * P], source[:, b, t0 + k * P : t0 + (k + 1) * P], ident[:])
                tokens.append(xt)
            return tokens

        def inverse_spread(squares, scale, eps):
            root = moments.tile([P, squares.shape[-1]], F32, name="root")
            nc.scalar.activation(root[:], squares, ACT.Sqrt, scale=scale)
            nc.vector.tensor_scalar_add(root[:], root[:], eps)
            inverse = moments.tile([P, squares.shape[-1]], F32, name="inverse")
            nc.vector.reciprocal(inverse[:], root[:])
            return inverse

        def rms_count(source, t0):
            tokens = flip(source, t0)
            inverses[t0] = []
            for k0 in range(0, TB, PAIR):
                sums = moments.tile([P, PAIR], F32, name="sums")
                for j in range(PAIR):
                    junk = unread.tile([P, C], BF16, name="junk")
                    nc.scalar.activation(junk[:], tokens[k0 + j][:], ACT.Square, accum_out=sums[:, j : j + 1])
                inverses[t0].append(inverse_spread(sums[:], 1.0 / C, EPS_RMS))

        def rms_apply(source, t0, y):
            spread = bank(CHUNK, "spread")
            for k in range(TB):
                inverse = inverses[t0][k // PAIR][:, k % PAIR : k % PAIR + 1]
                nc.tensor.transpose(spread[:, k * P : (k + 1) * P], inverse.to_broadcast([P, P]), ident[:])
            for b in range(CB):
                nc.vector.tensor_tensor(y[:, b, t0 : t0 + CHUNK], source[:, b, t0 : t0 + CHUNK], spread[:], ALU.mult)

        def normalise(t0):
            tokens = flip(x, t0)
            normals[t0] = []
            for k0 in range(0, TB, PAIR):
                mean_var = moments.tile([P, PAIR, 2], F32, name="mean_var")
                for j in range(PAIR):
                    stats = moments.tile([P, 6], F32, name="stats")
                    nc.vector.bn_stats(stats[:], tokens[k0 + j][:])
                    nc.vector.bn_aggr(mean_var[:, j, :], stats[:])
                mean, variance = mean_var[:, :, 0], mean_var[:, :, 1]
                inverse = inverse_spread(variance, 1.0, EPS_LN)
                by_vector = flipped.tile([P, C], F32, name="normal")
                nc.vector.tensor_scalar(
                    by_vector[:], tokens[k0][:], mean_var[:, 0, 0:1], inverse[:, 0:1], ALU.subtract, ALU.mult
                )
                offset = moments.tile([P, PAIR], F32, name="offset")
                nc.vector.scalar_tensor_tensor(offset[:], mean, -1.0, inverse[:], ALU.mult, ALU.mult)
                by_scalar = flipped.tile([P, C], F32, name="normal")
                nc.scalar.activation(
                    by_scalar[:], tokens[k0 + 1][:], ACT.Identity, bias=offset[:, 1:2], scale=inverse[:, 1:2]
                )
                normals[t0].extend([by_vector, by_scalar])

        def gain_and_shift(t0, y, gain, shift):
            channels = [bank(CHUNK, "channels") for b in range(CB)]
            for k in range(TB):
                for b in range(CB):
                    nc.tensor.transpose(
                        channels[b][:, k * P : (k + 1) * P], normals[t0][k][:, b * P : (b + 1) * P], ident[:]
                    )
            for b in range(CB):
                nc.scalar.activation(
                    y[:, b, t0 : t0 + CHUNK], channels[b][:], ACT.Identity, bias=column(shift, b), scale=column(gain, b)
                )

        def values(t0):
            for m in range(CB):
                nc.scalar.activation(
                    v[:, m, t0 : t0 + CHUNK], project(w_v_sb, m, blocks(xn, t0, CHUNK))[:], ACT.Identity,
                    bias=column("b_v", m),
                )

        def outputs(t0):
            for m in range(CB):
                x1 = x[:, m, t0 : t0 + CHUNK]
                nc.vector.scalar_tensor_tensor(
                    x1, project(w_o_sb, m, blocks(v, t0, CHUNK))[:], column("b_o", m), x1, ALU.add, ALU.add
                )

        hs, x2s = {}, {}

        def first_layer(t0):
            hs[t0] = wide.tile([P, FB, CHUNK], BF16, name="h")
            for f in range(FB):
                nc.scalar.activation(
                    hs[t0][:, f, :], project(fc_w_sb, f, blocks(xn2, t0, CHUNK))[:], ACT.Gelu_apprx_tanh,
                    bias=column("fc_b", f),
                )

        def second_layer(t0):
            x2s[t0] = wide.tile([P, CB, CHUNK], BF16, name="x2")
            for m in range(CB):
                nc.vector.scalar_tensor_tensor(
                    x2s[t0][:, m, :], project(fcp_w_sb, m, blocks(hs[t0], 0, CHUNK))[:], column("fcp_b", m),
                    x[:, m, t0 : t0 + CHUNK], ALU.add, ALU.add,
                )

        def unembed(t0):
            for t in range(SB):
                logit = logits.tile([P, CHUNK], F32, name="logit")
                nc.vector.tensor_scalar_add(
                    logit[:], project(unembd_w_sb, t, blocks(x2s[t0], 0, CHUNK))[:], column("unembd_b", t)
                )
                nc.sync.dma_start(out[t * P : (t + 1) * P, t0 : t0 + CHUNK], logit[:])

        embedding_stages = [
            lambda s0: rms_count(emb_sb, s0),
            lambda s0: rms_apply(emb_sb, s0, e),
            project_table,
        ]
        token_stages = [
            lambda t0: rms_count(hidden_sb, t0),
            lambda t0: rms_apply(hidden_sb, t0, u),
            look_up,
            normalise,
            lambda t0: gain_and_shift(t0, xn, "ln1_a", "ln1_b"),
            values,
            outputs,
            normalise,
            lambda t0: gain_and_shift(t0, xn2, "ln2_a", "ln2_b"),
            first_layer,
            second_layer,
            unembed,
        ]
        lanes = [(embedding_stages, 0, 0), (embedding_stages, CHUNK, 1)]
        lanes += [(token_stages, t0, 1 + i) for i, t0 in enumerate(chunks)]
        first_normalise = 1 + token_stages.index(normalise)
        for step in range(lanes[-1][2] + len(token_stages)):
            if step == first_normalise:
                turn_rows()
            for stages, c0, first_step in lanes:
                if 0 <= step - first_step < len(stages):
                    stages[step - first_step](c0)
